import numpy as np
import ml_dtypes


def mxq(x, axis, fmt="e4m3"):
    dtype, down = {"e4m3": (ml_dtypes.float8_e4m3fn, 7), "e5m2": (ml_dtypes.float8_e5m2, 14)}[fmt]
    v = np.moveaxis(np.asarray(x, np.float32).astype(ml_dtypes.bfloat16).astype(np.float64), axis, -1)
    blocks = v.reshape(v.shape[:-1] + (-1, 32))
    amax = np.abs(blocks).max(-1, keepdims=True)
    byte = np.maximum(np.where(amax > 0, np.frexp(amax)[1] - 1 + 127, 0) - down, 1)
    scale = np.exp2(byte - 127.0)
    codes = (blocks / scale).astype(np.float32).astype(dtype).astype(np.float64)
    return np.moveaxis((codes * scale).reshape(v.shape), -1, axis)


WIDE = False


def mx_kscale(k):
    if not WIDE:
        return np.ones(k)
    levels = np.array([10, -10, 5, -5, 0])
    if k % 512:
        return np.exp2(np.random.permutation(np.resize(levels, k // 32))).repeat(32)
    a = np.empty((k // 512, 16))
    for p in range(k // 512):
        a[p, :8] = np.random.permutation(np.resize(levels, 8))
        for g in range(8):
            far = levels[np.abs(levels - a[p, g]) >= 10]
            a[p, g + 8] = far[np.random.randint(len(far))]
    return np.exp2(a.ravel()).repeat(32)


BF16 = ml_dtypes.bfloat16


def bf(x):
    return np.asarray(x, np.float32).astype(BF16)


def f64(x):
    return np.asarray(x).astype(np.float64)


B, L, D, H, P, W = 2, 2048, 512, 4, 128, 128
HD = D // H
LT = L + P


def rotate_half(t):
    h = t.shape[-1] // 2
    return np.concatenate([-t[..., h:], t[..., :h]], axis=-1)


def project(pq, xq, w):
    wm = mxq(f64(w), 0, "e4m3")
    tp = pq @ wm
    tx = xq @ wm
    return np.concatenate([np.broadcast_to(tp, (B, P, D)), tx], axis=1).reshape(B, LT, H, HD)


def setup_inputs():
    s = mx_kscale(D)
    return {"x": bf(np.random.standard_normal((B, L, D)) * s),
            "pmem": bf(np.random.standard_normal((1, P, D)) * s),
            "cos": bf(np.random.uniform(size=(LT, HD))),
            "sin": bf(np.random.uniform(size=(LT, HD))),
            "wq": bf(np.random.standard_normal((D, D)) / np.sqrt(D) / s[:, None]),
            "wk": bf(np.random.standard_normal((D, D)) / np.sqrt(D) / s[:, None]),
            "wv": bf(np.random.standard_normal((D, D)) / np.sqrt(D) / s[:, None])}


def reference(x, pmem, cos, sin, wq, wk, wv):
    pq = mxq(f64(pmem), 2, "e4m3")
    xq = mxq(f64(x), 2, "e4m3")
    q = project(pq, xq, wq)
    k = project(pq, xq, wk)
    v = project(pq, xq, wv)
    cc = f64(cos)[None, :, None, :]
    ss = f64(sin)[None, :, None, :]
    q = q * cc + rotate_half(q) * ss
    k = k * cc + rotate_half(k) * ss
    return q, k, v

@@ -1,0 +1,265 @@
+from contextlib import ExitStack
+
+import concourse.mybir as mybir
+from concourse.masks import make_identity
+
+F32 = mybir.dt.float32
+BF16 = mybir.dt.bfloat16
+U32 = mybir.dt.uint32
+U8 = mybir.dt.uint8
+FP8X4 = mybir.dt.float8_e4m3fn_x4
+MULT = mybir.AluOpType.mult
+ADD = mybir.AluOpType.add
+
+P = 128
+PACK = 4
+B = 2
+L = 2048
+D = 512
+H = 4
+HD = D // H
+HALF = HD // 2
+GROUP = 4
+GROUP_TOKENS = GROUP * P
+GROUPS_PER_SEQ = L // GROUP_TOKENS
+TABLE_SLOTS = GROUPS_PER_SEQ * GROUP + 1
+TOKEN_TILES = B * GROUPS_PER_SEQ * GROUP + 1
+WORDS = D // 2
+ADD_TILES = 2
+FIRST = 0
+SECOND = 1
+V = 2
+BANK_TAGS = ("first", "second", "v")
+
+FLOPS = 2 * B * (L + P) * D * 3 * D
+
+
+def token_groups(x, pmem):
+    groups = [
+        {
+            "rows": pmem[0],
+            "tiles": 1,
+            "slot": GROUPS_PER_SEQ * GROUP,
+            "table_row": 0,
+            "loads_tables": True,
+            "stores": [(b, 0) for b in range(B)],
+        }
+    ]
+    for b in range(B):
+        for g in range(GROUPS_PER_SEQ):
+            row = g * GROUP_TOKENS
+            groups.append(
+                {
+                    "rows": x[b, row : row + GROUP_TOKENS, :],
+                    "tiles": GROUP,
+                    "slot": g * GROUP,
+                    "table_row": P + row,
+                    "loads_tables": b == 0,
+                    "stores": [(b, P + row)],
+                }
+            )
+    first_tile = 0
+    for group in groups:
+        group["first_tile"] = first_tile
+        first_tile += group["tiles"]
+    return groups
+
+
+def tile_titanstnt_pa_t_kernel(tc, x, pmem, cos, sin, wq, wk, wv, out_0, out_1, out_2):
+    nc = tc.nc
+    groups = token_groups(x, pmem)
+
+    with ExitStack() as ctx:
+        keep = ctx.enter_context(tc.tile_pool(name="keep", bufs=1))
+        stage = ctx.enter_context(tc.tile_pool(name="stage", bufs=2))
+        results = ctx.enter_context(tc.tile_pool(name="results", bufs=3))
+        psum = ctx.enter_context(tc.psum_pool(name="psum", bufs=2))
+        ctx.enter_context(tc.manual_schedule())
+
+        x_all = keep.tile([P, TOKEN_TILES * D], BF16)
+        x_words = x_all[:].bitcast(F32)
+        cos_sb = keep.tile([P, TABLE_SLOTS, HD], BF16)
+        sin_sb = keep.tile([P, TABLE_SLOTS, HD], BF16)
+        w_raw = keep.tile([P, 3, PACK, D], BF16)
+        w_grouped = keep.tile([P, 3, D, PACK], BF16, align_bytes=64)
+        w_codes = keep.tile([P, 3, D], U32, align_bytes=64)
+        w_scales = keep.tile([P, 3, D], U8, align_bytes=64)
+        identity = keep.tile([P, P], F32)
+
+        def load_weight(index, w):
+            nc.sync.dma_start(
+                out=w_raw[:, index].rearrange("p t c -> p (t c)"),
+                in_=w.rearrange("(p t) c -> p (t c)", t=PACK),
+            )
+
+        def load_group(group):
+            n = group["tiles"]
+            start = group["first_tile"] * D
+            nc.sync.dma_start(
+                out=x_all[:, start : start + n * D],
+                in_=group["rows"].rearrange("(p j) k -> p (j k)", j=n),
+            )
+            if group["loads_tables"]:
+                for table_sb, table in ((cos_sb, cos), (sin_sb, sin)):
+                    nc.sync.dma_start(
+                        out=table_sb[:, group["slot"] : group["slot"] + n, :],
+                        in_=table[group["table_row"] : group["table_row"] + n * P, :].rearrange(
+                            "(p j) d -> p j d", j=n
+                        ),
+                    )
+
+        load_weight(0, wq)
+        load_weight(1, wk)
+        load_group(groups[0])
+        load_weight(V, wv)
+        for group in groups[1:]:
+            load_group(group)
+
+        make_identity(nc, identity[:])
+
+        def transpose_tokens(group):
+            n = group["tiles"]
+            grouped = stage.tile([P, GROUP * P * PACK], BF16, align_bytes=64)
+            grouped_words = grouped[:].bitcast(F32)
+            for i0 in range(0, n, 2):
+                m = min(2, n - i0)
+                xt = psum.tile([P, 2, 2, P], F32)
+                for i in range(m):
+                    for u in range(2):
+                        start = (group["first_tile"] + i0 + i) * WORDS
+                        nc.tensor.transpose(xt[:, i, u, :], x_words[:, start + u : start + WORDS : 2], identity[:])
+                nc.scalar.copy(
+                    out=grouped_words[:, i0 * 2 * P : (i0 + m) * 2 * P].rearrange(
+                        "p (i r u) -> p i r u", i=m, u=2
+                    ),
+                    in_=xt[:, 0:m].rearrange("p i u r -> p i r u"),
+                )
+            if group["loads_tables"]:
+                minus = sin_sb[:, group["slot"] : group["slot"] + n, 0:HALF]
+                nc.scalar.mul(out=minus, in_=minus, mul=-1.0)
+            return grouped
+
+        def quantise_tokens(group, grouped):
+            n = group["tiles"]
+            x_codes = stage.tile([P, GROUP * P], U32, align_bytes=64)
+            x_scales = stage.tile([P, GROUP * P], U8, align_bytes=64)
+            nc.vector.quantize_mx(
+                out=x_codes[:, : n * P].bitcast(FP8X4),
+                scales=x_scales[:, : n * P],
+                in_=grouped[:, : n * P * PACK],
+            )
+            return x_codes, x_scales
+
+        def quantise_weights(bank):
+            nc.vector.quantize_mx(
+                out=w_codes[:, bank].bitcast(FP8X4),
+                scales=w_scales[:, bank],
+                in_=w_grouped[:, bank].rearrange("p c t -> p (c t)"),
+            )
+
+        def group_weight(index):
+            by_half = w_raw[:, index].rearrange("p t (h s d) -> p s h d t", s=2, d=HALF)
+            for half, copy in ((FIRST, nc.vector.tensor_copy), (SECOND, nc.scalar.copy)):
+                if index == V:
+                    sorted_columns = w_grouped[:, V].rearrange("p (h s d) t -> p s h d t", s=2, d=HALF)[:, half]
+                else:
+                    sorted_columns = w_grouped[:, half, index * H * HALF : (index + 1) * H * HALF, :].rearrange(
+                        "p (h d) t -> p h d t", h=H
+                    )
+                copy(out=sorted_columns, in_=by_half[:, half])
+
+        group_weight(0)
+        group_weight(1)
+        quantise_weights(FIRST)
+        quantise_weights(SECOND)
+
+        grouped = transpose_tokens(groups[0])
+        x_codes, x_scales = quantise_tokens(groups[0], grouped)
+
+        group_weight(V)
+        quantise_weights(V)
+
+        def heads(bank):
+            return bank[:].rearrange("p (q h d) -> p q h d", q=2, h=H)
+
+        def half_of(product, i, half):
+            return product[:, :, i, :].rearrange("p q (h s d) -> p q h s d", s=2, d=HALF)[:, :, :, half, :]
+
+        def table_half(table_sb, slot, half):
+            one = table_sb[:, slot, half * HALF : (half + 1) * HALF]
+            return one.unsqueeze(1).unsqueeze(1).to_broadcast([P, 2, H, HALF])
+
+        def store(group, out, result, i0, i1):
+            n = group["tiles"]
+            for b, row in group["stores"]:
+                nc.sync.dma_start(
+                    out=out[b, row : row + n * P].rearrange("(p j) h d -> p j (h d)", j=n)[:, i0:i1, :],
+                    in_=result[:, i0:i1, :],
+                )
+
+        def add_and_store(engine, group, by_cos, by_sin, i0, i1):
+            engine.tensor_tensor(
+                out=by_cos[:, :, i0:i1, :], in0=by_cos[:, :, i0:i1, :], in1=by_sin[:, :, i0:i1, :], op=ADD
+            )
+            store(group, out_0, by_cos[:, 0], i0, i1)
+            store(group, out_1, by_cos[:, 1], i0, i1)
+
+        for index, group in enumerate(groups):
+            n = group["tiles"]
+            following = groups[index + 1] if index + 1 < len(groups) else None
+            by_cos = results.tile([P, 2, GROUP, D], F32)
+            by_sin = stage.tile([P, 2, GROUP, D], F32)
+            v_sb = results.tile([P, GROUP, D], F32)
+
+            span = ADD_TILES if following is not None else 1
+            gpsimd_tiles = n if following is not None else n - ADD_TILES
+
+            for i in range(n):
+                columns = slice(i * P, (i + 1) * P)
+                banks = []
+                for bank in (FIRST, SECOND, V):
+                    if bank == V and i == 0 and following is not None:
+                        grouped = transpose_tokens(following)
+                    acc = psum.tile([P, D], F32, name=BANK_TAGS[bank])
+                    nc.tensor.matmul_mx(
+                        out=acc[:],
+                        lhsT=x_codes[:, columns].bitcast(FP8X4),
+                        lhsT_scale=x_scales[:, columns],
+                        rhs=w_codes[:, bank].bitcast(FP8X4),
+                        rhs_scale=w_scales[:, bank],
+                        start=True,
+                        stop=True,
+                    )
+                    banks.append(acc)
+
+                slot = group["slot"] + i
+                for bank, cos_half in ((FIRST, 0), (SECOND, 1)):
+                    nc.vector.tensor_tensor(
+                        out=half_of(by_cos, i, cos_half),
+                        in0=heads(banks[bank]),
+                        in1=table_half(cos_sb, slot, cos_half),
+                        op=MULT,
+                    )
+                    nc.vector.tensor_tensor(
+                        out=half_of(by_sin, i, 1 - cos_half),
+                        in0=heads(banks[bank]),
+                        in1=table_half(sin_sb, slot, 1 - cos_half),
+                        op=MULT,
+                    )
+
+                nc.scalar.copy(out=v_sb[:, i, :], in_=banks[V][:])
+
+                if i == min(ADD_TILES, n) - 1 and following is not None:
+                    next_codes, next_scales = quantise_tokens(following, grouped)
+
+                if (i + 1) % span == 0 or i == n - 1:
+                    i0 = i - i % span
+                    store(group, out_2, v_sb, i0, i + 1)
+                    if i0 < gpsimd_tiles:
+                        add_and_store(nc.gpsimd, group, by_cos, by_sin, i0, i + 1)
+
+            for i in range(gpsimd_tiles, n):
+                add_and_store(nc.vector, group, by_cos, by_sin, i, i + 1)
+
+            if following is not None:
+                x_codes, x_scales = next_codes, next_scales

@@ -25,11 +25,8 @@ GROUPS_PER_SEQ = L // GROUP_TOKENS
 TABLE_SLOTS = GROUPS_PER_SEQ * GROUP + 1
 TOKEN_TILES = B * GROUPS_PER_SEQ * GROUP + 1
 WORDS = D // 2
-ADD_TILES = 2
-FIRST = 0
-SECOND = 1
-V = 2
-BANK_TAGS = ("first", "second", "v")
+STEP = 2
+Q, K, V = 0, 1, 2
 
 FLOPS = 2 * B * (L + P) * D * 3 * D
 
@@ -68,23 +65,34 @@ def token_groups(x, pmem):
 def tile_titanstnt_pa_t_kernel(tc, x, pmem, cos, sin, wq, wk, wv, out_0, out_1, out_2):
     nc = tc.nc
     groups = token_groups(x, pmem)
+    steps = []
+    for index, group in enumerate(groups):
+        for half in range(max(1, group["tiles"] // STEP)):
+            steps.append({"index": index, "group": group, "half": half, "tiles": min(STEP, group["tiles"])})
 
     with ExitStack() as ctx:
         keep = ctx.enter_context(tc.tile_pool(name="keep", bufs=1))
         stage = ctx.enter_context(tc.tile_pool(name="stage", bufs=2))
-        results = ctx.enter_context(tc.tile_pool(name="results", bufs=3))
+        kparts = ctx.enter_context(tc.tile_pool(name="kparts", bufs=4))
+        results = ctx.enter_context(tc.tile_pool(name="results", bufs=5))
+        kresults = ctx.enter_context(tc.tile_pool(name="kresults", bufs=3))
         psum = ctx.enter_context(tc.psum_pool(name="psum", bufs=2))
         ctx.enter_context(tc.manual_schedule())
 
         x_all = keep.tile([P, TOKEN_TILES * D], BF16)
         x_words = x_all[:].bitcast(F32)
         cos_sb = keep.tile([P, TABLE_SLOTS, HD], BF16)
+        sin_raw = keep.tile([P, TABLE_SLOTS, HD], BF16)
         sin_sb = keep.tile([P, TABLE_SLOTS, HD], BF16)
+        cos_t = keep.tile([P, TABLE_SLOTS * P], BF16)
+        sin_t = keep.tile([P, TABLE_SLOTS * P], BF16)
         w_raw = keep.tile([P, 3, PACK, D], BF16)
         w_grouped = keep.tile([P, 3, D, PACK], BF16, align_bytes=64)
         w_codes = keep.tile([P, 3, D], U32, align_bytes=64)
         w_scales = keep.tile([P, 3, D], U8, align_bytes=64)
         identity = keep.tile([P, P], F32)
+        swap = keep.tile([P, P], F32)
+        identity_bf = keep.tile([P, P], BF16)
 
         def load_weight(index, w):
             nc.sync.dma_start(
@@ -92,15 +100,18 @@ def tile_titanstnt_pa_t_kernel(tc, x, pmem, cos, sin, wq, wk, wv, out_0, out_1, 
                 in_=w.rearrange("(p t) c -> p (t c)", t=PACK),
             )
 
-        def load_group(group):
+        def load_tokens(group):
             n = group["tiles"]
             start = group["first_tile"] * D
             nc.sync.dma_start(
                 out=x_all[:, start : start + n * D],
                 in_=group["rows"].rearrange("(p j) k -> p (j k)", j=n),
             )
+
+        def load_tables(group):
+            n = group["tiles"]
             if group["loads_tables"]:
-                for table_sb, table in ((cos_sb, cos), (sin_sb, sin)):
+                for table_sb, table in ((cos_sb, cos), (sin_raw, sin)):
                     nc.sync.dma_start(
                         out=table_sb[:, group["slot"] : group["slot"] + n, :],
                         in_=table[group["table_row"] : group["table_row"] + n * P, :].rearrange(
@@ -108,35 +119,37 @@ def tile_titanstnt_pa_t_kernel(tc, x, pmem, cos, sin, wq, wk, wv, out_0, out_1, 
                         ),
                     )
 
-        load_weight(0, wq)
-        load_weight(1, wk)
-        load_group(groups[0])
+        load_tokens(groups[0])
+        load_weight(Q, wq)
+        load_tables(groups[0])
+        load_weight(K, wk)
         load_weight(V, wv)
-        for group in groups[1:]:
-            load_group(group)
+        load_tokens(groups[1])
+        load_tables(groups[1])
+        for group in groups[2:]:
+            load_tokens(group)
+            load_tables(group)
 
         make_identity(nc, identity[:])
+        make_identity(nc, identity_bf[:])
+        nc.gpsimd.tensor_copy(out=swap[:, 0:HALF], in_=identity[:, HALF:HD])
+        nc.gpsimd.tensor_copy(out=swap[:, HALF:HD], in_=identity[:, 0:HALF])
 
-        def transpose_tokens(group):
-            n = group["tiles"]
+        def transpose_tokens(group, grouped, i0, m):
+            xt = psum.tile([P, 2, 2, P], F32, name="misc")
+            for i in range(m):
+                for u in range(2):
+                    start = (group["first_tile"] + i0 + i) * WORDS
+                    nc.tensor.transpose(xt[:, i, u, :], x_words[:, start + u : start + WORDS : 2], identity[:])
+            nc.scalar.copy(
+                out=grouped[:].bitcast(F32)[:, i0 * 2 * P : (i0 + m) * 2 * P].rearrange(
+                    "p (i r u) -> p i r u", i=m, u=2
+                ),
+                in_=xt[:, 0:m].rearrange("p i u r -> p i r u"),
+            )
+
+        def new_grouped():
             grouped = stage.tile([P, GROUP * P * PACK], BF16, align_bytes=64)
-            grouped_words = grouped[:].bitcast(F32)
-            for i0 in range(0, n, 2):
-                m = min(2, n - i0)
-                xt = psum.tile([P, 2, 2, P], F32)
-                for i in range(m):
-                    for u in range(2):
-                        start = (group["first_tile"] + i0 + i) * WORDS
-                        nc.tensor.transpose(xt[:, i, u, :], x_words[:, start + u : start + WORDS : 2], identity[:])
-                nc.scalar.copy(
-                    out=grouped_words[:, i0 * 2 * P : (i0 + m) * 2 * P].rearrange(
-                        "p (i r u) -> p i r u", i=m, u=2
-                    ),
-                    in_=xt[:, 0:m].rearrange("p i u r -> p i r u"),
-                )
-            if group["loads_tables"]:
-                minus = sin_sb[:, group["slot"] : group["slot"] + n, 0:HALF]
-                nc.scalar.mul(out=minus, in_=minus, mul=-1.0)
             return grouped
 
         def quantise_tokens(group, grouped):
@@ -150,116 +163,258 @@ def tile_titanstnt_pa_t_kernel(tc, x, pmem, cos, sin, wq, wk, wv, out_0, out_1, 
             )
             return x_codes, x_scales
 
-        def quantise_weights(bank):
-            nc.vector.quantize_mx(
-                out=w_codes[:, bank].bitcast(FP8X4),
-                scales=w_scales[:, bank],
-                in_=w_grouped[:, bank].rearrange("p c t -> p (c t)"),
-            )
+        def prepare_tables(group):
+            n, slot = group["tiles"], group["slot"]
+            slots = slice(slot, slot + n)
+            for half, sign in ((0, 1.0), (1, -1.0)):
+                nc.gpsimd.tensor_scalar(
+                    out=sin_sb[:, slots, half * HALF : (half + 1) * HALF],
+                    in0=sin_raw[:, slots, (1 - half) * HALF : (2 - half) * HALF],
+                    scalar1=sign,
+                    scalar2=0.0,
+                    op0=MULT,
+                    op1=ADD,
+                )
+
+        def transpose_tables(group):
+            n, slot = group["tiles"], group["slot"]
+            tt = psum.tile([P, 2, GROUP, P], BF16, name="misc")
+            for i in range(n):
+                nc.tensor.transpose(tt[:, 0, i, :], cos_sb[:, slot + i, :], identity_bf[:])
+            for i in range(n):
+                nc.tensor.transpose(tt[:, 1, i, :], sin_sb[:, slot + i, :], identity_bf[:])
+            columns = slice(slot * P, (slot + n) * P)
+            nc.scalar.copy(out=cos_t[:, columns].rearrange("p (i r) -> p i r", i=n), in_=tt[:, 0, 0:n, :])
+            nc.scalar.copy(out=sin_t[:, columns].rearrange("p (i r) -> p i r", i=n), in_=tt[:, 1, 0:n, :])
 
         def group_weight(index):
-            by_half = w_raw[:, index].rearrange("p t (h s d) -> p s h d t", s=2, d=HALF)
-            for half, copy in ((FIRST, nc.vector.tensor_copy), (SECOND, nc.scalar.copy)):
-                if index == V:
-                    sorted_columns = w_grouped[:, V].rearrange("p (h s d) t -> p s h d t", s=2, d=HALF)[:, half]
-                else:
-                    sorted_columns = w_grouped[:, half, index * H * HALF : (index + 1) * H * HALF, :].rearrange(
-                        "p (h d) t -> p h d t", h=H
+            for columns, copy in ((slice(0, D // 2), nc.vector.tensor_copy), (slice(D // 2, D), nc.scalar.copy)):
+                copy(
+                    out=w_grouped[:, index, columns, :],
+                    in_=w_raw[:, index, :, columns].rearrange("p t c -> p c t"),
+                )
+
+        def quantise_weights(index):
+            nc.vector.quantize_mx(
+                out=w_codes[:, index].bitcast(FP8X4),
+                scales=w_scales[:, index],
+                in_=w_grouped[:, index].rearrange("p c t -> p (c t)"),
+            )
+
+        def project(step, tile, index, acc):
+            x_codes, x_scales = step["group"]["codes"]
+            columns = slice(tile * P, (tile + 1) * P)
+            nc.tensor.matmul_mx(
+                out=acc[:],
+                lhsT=x_codes[:, columns].bitcast(FP8X4),
+                lhsT_scale=x_scales[:, columns],
+                rhs=w_codes[:, index].bitcast(FP8X4),
+                rhs_scale=w_scales[:, index],
+                start=True,
+                stop=True,
+            )
+
+        def project_head(step, head, out):
+            x_codes, x_scales = step["group"]["codes"]
+            n = step["group"]["tiles"]
+            columns = slice(head * HD, (head + 1) * HD)
+            nc.tensor.matmul_mx(
+                out=out,
+                lhsT=w_codes[:, K, columns].bitcast(FP8X4),
+                lhsT_scale=w_scales[:, K, columns],
+                rhs=x_codes[:, : n * P].bitcast(FP8X4),
+                rhs_scale=x_scales[:, : n * P],
+                start=True,
+                stop=True,
+            )
+
+        def start_k(step):
+            n = step["group"]["tiles"]
+            step["k_banks"] = []
+            if n == 1:
+                acc = psum.tile([P, GROUP * P], F32, name="kacc")
+                for head in range(H):
+                    project_head(step, head, acc[:, head * P : (head + 1) * P])
+                step["k_banks"].append(acc)
+            else:
+                for j in range(STEP):
+                    acc = psum.tile([P, GROUP * P], F32, name="kacc")
+                    project_head(step, step["half"] * STEP + j, acc[:])
+                    step["k_banks"].append(acc)
+
+        def on_gpsimd(step, j):
+            return step["group"]["tiles"] > 1 and step["half"] == 1 and j == 1
+
+        def copy_k_for_gpsimd(step):
+            for j, acc in enumerate(step["k_banks"]):
+                if on_gpsimd(step, j):
+                    k_copy = stage.tile([P, GROUP * P], F32)
+                    nc.scalar.copy(out=k_copy[:], in_=acc[:])
+                    step["k_copy"] = k_copy
+
+        def multiply_k(step, gpsimd):
+            n, slot = step["group"]["tiles"], step["group"]["slot"]
+            columns = slice(slot * P, (slot + n) * P)
+            if "k_parts" not in step:
+                step["k_parts"] = [None for acc in step["k_banks"]]
+            for j, acc in enumerate(step["k_banks"]):
+                if on_gpsimd(step, j) != gpsimd:
+                    continue
+                by_cos_t = kparts.tile([P, GROUP * P], F32)
+                by_sin_t = kparts.tile([P, GROUP * P], F32)
+                source = step["k_copy"] if gpsimd else acc
+                engine = nc.gpsimd if gpsimd else nc.vector
+                for part, table in ((by_cos_t, cos_t), (by_sin_t, sin_t)):
+                    values = table[:, columns]
+                    if n == 1:
+                        engine.tensor_tensor(
+                            out=part[:].rearrange("p (h r) -> p h r", h=H),
+                            in0=source[:].rearrange("p (h r) -> p h r", h=H),
+                            in1=values.unsqueeze(1).to_broadcast([P, H, P]),
+                            op=MULT,
+                        )
+                    else:
+                        engine.tensor_tensor(out=part[:], in0=source[:], in1=values, op=MULT)
+                step["k_parts"][j] = (by_cos_t, by_sin_t)
+
+        def add_k(step):
+            group = step["group"]
+            if step["half"] == 0:
+                group["k_sb"] = kresults.tile([P, GROUP, D], F32, name="k_sb")
+            for j, (by_cos_t, by_sin_t) in enumerate(step["k_parts"]):
+                ko = psum.tile([P, GROUP, P], F32)
+                for i in range(GROUP):
+                    columns = slice(i * P, (i + 1) * P)
+                    nc.tensor.matmul(
+                        ko[:, i, :], lhsT=by_cos_t[:, columns], rhs=identity[:], start=True, stop=False, is_transpose=True
                     )
-                copy(out=sorted_columns, in_=by_half[:, half])
+                    nc.tensor.matmul(
+                        ko[:, i, :], lhsT=by_sin_t[:, columns], rhs=swap[:], start=False, stop=True, is_transpose=True
+                    )
+                if group["tiles"] == 1:
+                    nc.scalar.copy(out=group["k_sb"][:, 0, :].rearrange("p (h d) -> p h d", h=H), in_=ko[:])
+                else:
+                    head = step["half"] * STEP + j
+                    nc.scalar.copy(out=group["k_sb"][:, :, head * HD : (head + 1) * HD], in_=ko[:])
 
-        group_weight(0)
-        group_weight(1)
-        quantise_weights(FIRST)
-        quantise_weights(SECOND)
+        def start_q(step):
+            step["q_banks"] = []
+            for i in range(step["tiles"]):
+                acc = psum.tile([P, D], F32, name="qacc")
+                project(step, step["half"] * STEP + i, Q, acc)
+                step["q_banks"].append(acc)
 
-        grouped = transpose_tokens(groups[0])
-        x_codes, x_scales = quantise_tokens(groups[0], grouped)
+        def multiply_q(step, i):
+            if i == 0:
+                by_cos = results.tile([P, STEP, D], F32)
+                by_sin = results.tile([P, STEP, D], F32)
+                step["q_parts"] = (by_cos, by_sin)
+            by_cos, by_sin = step["q_parts"]
+            if i < step["tiles"]:
+                acc = step["q_banks"][i]
+                slot = step["group"]["slot"] + step["half"] * STEP + i
+                for part, table in ((by_cos, cos_sb), (by_sin, sin_sb)):
+                    nc.vector.tensor_tensor(
+                        out=part[:, i, :].rearrange("p (h d) -> p h d", h=H),
+                        in0=acc[:].rearrange("p (h d) -> p h d", h=H),
+                        in1=table[:, slot, :].unsqueeze(1).to_broadcast([P, H, HD]),
+                        op=MULT,
+                    )
 
-        group_weight(V)
-        quantise_weights(V)
+        def add_q(step, engine):
+            n = step["tiles"]
+            by_cos, by_sin = step["q_parts"]
+            cos_halves = by_cos[:, 0:n, :].rearrange("p i (h s d) -> p i h s d", h=H, s=2)
+            sin_halves = by_sin[:, 0:n, :].rearrange("p i (h s d) -> p i h s d", h=H, s=2)
+            for s in range(2):
+                engine.tensor_tensor(
+                    out=cos_halves[:, :, :, s, :], in0=cos_halves[:, :, :, s, :], in1=sin_halves[:, :, :, 1 - s, :], op=ADD
+                )
 
-        def heads(bank):
-            return bank[:].rearrange("p (q h d) -> p q h d", q=2, h=H)
-
-        def half_of(product, i, half):
-            return product[:, :, i, :].rearrange("p q (h s d) -> p q h s d", s=2, d=HALF)[:, :, :, half, :]
-
-        def table_half(table_sb, slot, half):
-            one = table_sb[:, slot, half * HALF : (half + 1) * HALF]
-            return one.unsqueeze(1).unsqueeze(1).to_broadcast([P, 2, H, HALF])
-
-        def store(group, out, result, i0, i1):
+        def store(group, out, result, i0, m):
             n = group["tiles"]
             for b, row in group["stores"]:
                 nc.sync.dma_start(
-                    out=out[b, row : row + n * P].rearrange("(p j) h d -> p j (h d)", j=n)[:, i0:i1, :],
-                    in_=result[:, i0:i1, :],
+                    out=out[b, row : row + n * P].rearrange("(p j) h d -> p j (h d)", j=n)[:, i0 : i0 + m, :],
+                    in_=result[:, 0:m, :],
                 )
 
-        def add_and_store(engine, group, by_cos, by_sin, i0, i1):
-            engine.tensor_tensor(
-                out=by_cos[:, :, i0:i1, :], in0=by_cos[:, :, i0:i1, :], in1=by_sin[:, :, i0:i1, :], op=ADD
-            )
-            store(group, out_0, by_cos[:, 0], i0, i1)
-            store(group, out_1, by_cos[:, 1], i0, i1)
+        def project_v(step, i):
+            if i == 0:
+                step["v_sb"] = results.tile([P, STEP, D], F32, name="v_sb")
+            acc = psum.tile([P, D], F32, name="misc")
+            project(step, step["half"] * STEP + i, V, acc)
+            nc.scalar.copy(out=step["v_sb"][:, i, :], in_=acc[:])
 
-        for index, group in enumerate(groups):
-            n = group["tiles"]
-            following = groups[index + 1] if index + 1 < len(groups) else None
-            by_cos = results.tile([P, 2, GROUP, D], F32)
-            by_sin = stage.tile([P, 2, GROUP, D], F32)
-            v_sb = results.tile([P, GROUP, D], F32)
+        groups[0]["grouped"] = new_grouped()
+        transpose_tokens(groups[0], groups[0]["grouped"], 0, 1)
+        prepare_tables(groups[0])
+        group_weight(Q)
+        groups[0]["codes"] = quantise_tokens(groups[0], groups[0]["grouped"])
+        quantise_weights(Q)
+        start_q(steps[0])
+        transpose_tables(groups[0])
+        group_weight(K)
+        quantise_weights(K)
+        start_k(steps[0])
+        multiply_q(steps[0], 0)
+        group_weight(V)
+        groups[1]["grouped"] = new_grouped()
+        transpose_tokens(groups[1], groups[1]["grouped"], 0, STEP)
+        transpose_tokens(groups[1], groups[1]["grouped"], STEP, STEP)
+        prepare_tables(groups[1])
+        transpose_tables(groups[1])
+        multiply_k(steps[0], gpsimd=False)
+        groups[1]["codes"] = quantise_tokens(groups[1], groups[1]["grouped"])
+        start_k(steps[1])
+        copy_k_for_gpsimd(steps[1])
+        quantise_weights(V)
+        multiply_k(steps[1], gpsimd=True)
+        add_q(steps[0], nc.gpsimd)
+        project_v(steps[0], 0)
+        groups[2]["grouped"] = new_grouped()
+        transpose_tokens(groups[2], groups[2]["grouped"], 0, STEP)
+        prepare_tables(groups[2])
+        store(groups[0], out_2, steps[0]["v_sb"], 0, 1)
+        store(groups[0], out_0, steps[0]["q_parts"][0], 0, 1)
 
-            span = ADD_TILES if following is not None else 1
-            gpsimd_tiles = n if following is not None else n - ADD_TILES
+        for number, step in enumerate(steps):
+            if number == 0:
+                continue
+            group = step["group"]
+            before = steps[number - 1]
+            following = steps[number + 1] if number + 1 < len(steps) else None
+            next_group = groups[step["index"] + 1] if step["index"] + 1 < len(groups) else None
+            second_group = groups[step["index"] + 2] if step["index"] + 2 < len(groups) else None
+            second = step["half"] == 1
 
-            for i in range(n):
-                columns = slice(i * P, (i + 1) * P)
-                banks = []
-                for bank in (FIRST, SECOND, V):
-                    if bank == V and i == 0 and following is not None:
-                        grouped = transpose_tokens(following)
-                    acc = psum.tile([P, D], F32, name=BANK_TAGS[bank])
-                    nc.tensor.matmul_mx(
-                        out=acc[:],
-                        lhsT=x_codes[:, columns].bitcast(FP8X4),
-                        lhsT_scale=x_scales[:, columns],
-                        rhs=w_codes[:, bank].bitcast(FP8X4),
-                        rhs_scale=w_scales[:, bank],
-                        start=True,
-                        stop=True,
-                    )
-                    banks.append(acc)
-
-                slot = group["slot"] + i
-                for bank, cos_half in ((FIRST, 0), (SECOND, 1)):
-                    nc.vector.tensor_tensor(
-                        out=half_of(by_cos, i, cos_half),
-                        in0=heads(banks[bank]),
-                        in1=table_half(cos_sb, slot, cos_half),
-                        op=MULT,
-                    )
-                    nc.vector.tensor_tensor(
-                        out=half_of(by_sin, i, 1 - cos_half),
-                        in0=heads(banks[bank]),
-                        in1=table_half(sin_sb, slot, 1 - cos_half),
-                        op=MULT,
-                    )
-
-                nc.scalar.copy(out=v_sb[:, i, :], in_=banks[V][:])
-
-                if i == min(ADD_TILES, n) - 1 and following is not None:
-                    next_codes, next_scales = quantise_tokens(following, grouped)
-
-                if (i + 1) % span == 0 or i == n - 1:
-                    i0 = i - i % span
-                    store(group, out_2, v_sb, i0, i + 1)
-                    if i0 < gpsimd_tiles:
-                        add_and_store(nc.gpsimd, group, by_cos, by_sin, i0, i + 1)
-
-            for i in range(gpsimd_tiles, n):
-                add_and_store(nc.vector, group, by_cos, by_sin, i, i + 1)
-
+            multiply_k(step, gpsimd=False)
+            start_q(step)
+            multiply_q(step, 0)
+            if second and next_group is not None:
+                next_group["codes"] = quantise_tokens(next_group, next_group["grouped"])
+            add_k(before)
+            if before["half"] == 1 or number == 1:
+                store(before["group"], out_1, before["group"]["k_sb"], 0, before["group"]["tiles"])
+            if not second and next_group is not None:
+                transpose_tokens(next_group, next_group["grouped"], STEP, STEP)
+            if second and second_group is not None:
+                second_group["grouped"] = new_grouped()
+                transpose_tokens(second_group, second_group["grouped"], 0, STEP)
+            if next_group is not None and next_group["loads_tables"] and not second:
+                transpose_tables(next_group)
             if following is not None:
-                x_codes, x_scales = next_codes, next_scales
+                start_k(following)
+                copy_k_for_gpsimd(following)
+            if second and second_group is not None and second_group["loads_tables"]:
+                prepare_tables(second_group)
+            if following is not None:
+                multiply_k(following, gpsimd=True)
+            project_v(step, 0)
+            project_v(step, 1)
+            multiply_q(step, 1)
+            add_q(step, nc.gpsimd if following is not None else nc.vector)
+            store(group, out_2, step["v_sb"], step["half"] * STEP, step["tiles"])
+            store(group, out_0, step["q_parts"][0], step["half"] * STEP, step["tiles"])
+        add_k(steps[-1])
+        store(groups[-1], out_1, groups[-1]["k_sb"], 0, GROUP)

@@ -25,8 +25,10 @@ GROUPS_PER_SEQ = L // GROUP_TOKENS
 TABLE_SLOTS = GROUPS_PER_SEQ * GROUP + 1
 TOKEN_TILES = B * GROUPS_PER_SEQ * GROUP + 1
 WORDS = D // 2
-STEP = 2
+PAIR = 2
 Q, K, V = 0, 1, 2
+VECTOR_COLUMNS = 320
+GPSIMD_ROWS = ((), (), (), (0, 1))
 
 FLOPS = 2 * B * (L + P) * D * 3 * D
 
@@ -65,10 +67,11 @@ def token_groups(x, pmem):
 def tile_titanstnt_pa_t_kernel(tc, x, pmem, cos, sin, wq, wk, wv, out_0, out_1, out_2):
     nc = tc.nc
     groups = token_groups(x, pmem)
-    steps = []
-    for index, group in enumerate(groups):
-        for half in range(max(1, group["tiles"] // STEP)):
-            steps.append({"index": index, "group": group, "half": half, "tiles": min(STEP, group["tiles"])})
+    units = [
+        {"index": index, "group": group, "part": part}
+        for index, group in enumerate(groups)
+        for part in range(group["tiles"])
+    ]
 
     with ExitStack() as ctx:
         keep = ctx.enter_context(tc.tile_pool(name="keep", bufs=1))
@@ -81,11 +84,9 @@ def tile_titanstnt_pa_t_kernel(tc, x, pmem, cos, sin, wq, wk, wv, out_0, out_1, 
 
         x_all = keep.tile([P, TOKEN_TILES * D], BF16)
         x_words = x_all[:].bitcast(F32)
-        cos_sb = keep.tile([P, TABLE_SLOTS, HD], BF16)
+        tables = keep.tile([P, 2, TABLE_SLOTS, HD], BF16)
         sin_raw = keep.tile([P, TABLE_SLOTS, HD], BF16)
-        sin_sb = keep.tile([P, TABLE_SLOTS, HD], BF16)
-        cos_t = keep.tile([P, TABLE_SLOTS * P], BF16)
-        sin_t = keep.tile([P, TABLE_SLOTS * P], BF16)
+        tables_t = keep.tile([P, 2, TABLE_SLOTS * P], BF16)
         w_raw = keep.tile([P, 3, PACK, D], BF16)
         w_grouped = keep.tile([P, 3, D, PACK], BF16, align_bytes=64)
         w_codes = keep.tile([P, 3, D], U32, align_bytes=64)
@@ -111,9 +112,10 @@ def tile_titanstnt_pa_t_kernel(tc, x, pmem, cos, sin, wq, wk, wv, out_0, out_1, 
         def load_tables(group):
             n = group["tiles"]
             if group["loads_tables"]:
-                for table_sb, table in ((cos_sb, cos), (sin_raw, sin)):
+                slots = slice(group["slot"], group["slot"] + n)
+                for table_sb, table in ((tables[:, 0, slots, :], cos), (sin_raw[:, slots, :], sin)):
                     nc.sync.dma_start(
-                        out=table_sb[:, group["slot"] : group["slot"] + n, :],
+                        out=table_sb,
                         in_=table[group["table_row"] : group["table_row"] + n * P, :].rearrange(
                             "(p j) d -> p j d", j=n
                         ),
@@ -135,25 +137,20 @@ def tile_titanstnt_pa_t_kernel(tc, x, pmem, cos, sin, wq, wk, wv, out_0, out_1, 
         nc.gpsimd.tensor_copy(out=swap[:, 0:HALF], in_=identity[:, HALF:HD])
         nc.gpsimd.tensor_copy(out=swap[:, HALF:HD], in_=identity[:, 0:HALF])
 
-        def transpose_tokens(group, grouped, i0, m):
-            xt = psum.tile([P, 2, 2, P], F32, name="misc")
-            for i in range(m):
-                for u in range(2):
-                    start = (group["first_tile"] + i0 + i) * WORDS
-                    nc.tensor.transpose(xt[:, i, u, :], x_words[:, start + u : start + WORDS : 2], identity[:])
+        def transpose_tokens(group, i):
+            if i == 0:
+                group["grouped"] = stage.tile([P, GROUP * P * PACK], BF16, align_bytes=64, name="grouped")
+            xt = psum.tile([P, 2, P], F32, name="misc")
+            for u in range(2):
+                start = (group["first_tile"] + i) * WORDS
+                nc.tensor.transpose(xt[:, u, :], x_words[:, start + u : start + WORDS : 2], identity[:])
             nc.scalar.copy(
-                out=grouped[:].bitcast(F32)[:, i0 * 2 * P : (i0 + m) * 2 * P].rearrange(
-                    "p (i r u) -> p i r u", i=m, u=2
-                ),
-                in_=xt[:, 0:m].rearrange("p i u r -> p i r u"),
+                out=group["grouped"][:].bitcast(F32)[:, i * 2 * P : (i + 1) * 2 * P].rearrange("p (r u) -> p r u", u=2),
+                in_=xt[:].rearrange("p u r -> p r u"),
             )
 
-        def new_grouped():
-            grouped = stage.tile([P, GROUP * P * PACK], BF16, align_bytes=64)
-            return grouped
-
-        def quantise_tokens(group, grouped):
-            n = group["tiles"]
+        def quantise_tokens(group):
+            n, grouped = group["tiles"], group["grouped"]
             x_codes = stage.tile([P, GROUP * P], U32, align_bytes=64)
             x_scales = stage.tile([P, GROUP * P], U8, align_bytes=64)
             nc.vector.quantize_mx(
@@ -161,14 +158,14 @@ def tile_titanstnt_pa_t_kernel(tc, x, pmem, cos, sin, wq, wk, wv, out_0, out_1, 
                 scales=x_scales[:, : n * P],
                 in_=grouped[:, : n * P * PACK],
             )
-            return x_codes, x_scales
+            group["codes"] = (x_codes, x_scales)
 
         def prepare_tables(group):
             n, slot = group["tiles"], group["slot"]
             slots = slice(slot, slot + n)
             for half, sign in ((0, 1.0), (1, -1.0)):
                 nc.gpsimd.tensor_scalar(
-                    out=sin_sb[:, slots, half * HALF : (half + 1) * HALF],
+                    out=tables[:, 1, slots, half * HALF : (half + 1) * HALF],
                     in0=sin_raw[:, slots, (1 - half) * HALF : (2 - half) * HALF],
                     scalar1=sign,
                     scalar2=0.0,
@@ -179,16 +176,19 @@ def tile_titanstnt_pa_t_kernel(tc, x, pmem, cos, sin, wq, wk, wv, out_0, out_1, 
         def transpose_tables(group):
             n, slot = group["tiles"], group["slot"]
             tt = psum.tile([P, 2, GROUP, P], BF16, name="misc")
-            for i in range(n):
-                nc.tensor.transpose(tt[:, 0, i, :], cos_sb[:, slot + i, :], identity_bf[:])
-            for i in range(n):
-                nc.tensor.transpose(tt[:, 1, i, :], sin_sb[:, slot + i, :], identity_bf[:])
+            for row in range(2):
+                for i in range(n):
+                    nc.tensor.transpose(tt[:, row, i, :], tables[:, row, slot + i, :], identity_bf[:])
             columns = slice(slot * P, (slot + n) * P)
-            nc.scalar.copy(out=cos_t[:, columns].rearrange("p (i r) -> p i r", i=n), in_=tt[:, 0, 0:n, :])
-            nc.scalar.copy(out=sin_t[:, columns].rearrange("p (i r) -> p i r", i=n), in_=tt[:, 1, 0:n, :])
+            nc.scalar.copy(
+                out=tables_t[:, :, columns].rearrange("p w (i r) -> p w i r", i=n), in_=tt[:, :, 0:n, :]
+            )
 
         def group_weight(index):
-            for columns, copy in ((slice(0, D // 2), nc.vector.tensor_copy), (slice(D // 2, D), nc.scalar.copy)):
+            for columns, copy in (
+                (slice(0, VECTOR_COLUMNS), nc.vector.tensor_copy),
+                (slice(VECTOR_COLUMNS, D), nc.scalar.copy),
+            ):
                 copy(
                     out=w_grouped[:, index, columns, :],
                     in_=w_raw[:, index, :, columns].rearrange("p t c -> p c t"),
@@ -201,9 +201,9 @@ def tile_titanstnt_pa_t_kernel(tc, x, pmem, cos, sin, wq, wk, wv, out_0, out_1, 
                 in_=w_grouped[:, index].rearrange("p c t -> p (c t)"),
             )
 
-        def project(step, tile, index, acc):
-            x_codes, x_scales = step["group"]["codes"]
-            columns = slice(tile * P, (tile + 1) * P)
+        def project(unit, index, acc):
+            x_codes, x_scales = unit["group"]["codes"]
+            columns = slice(unit["part"] * P, (unit["part"] + 1) * P)
             nc.tensor.matmul_mx(
                 out=acc[:],
                 lhsT=x_codes[:, columns].bitcast(FP8X4),
@@ -214,9 +214,9 @@ def tile_titanstnt_pa_t_kernel(tc, x, pmem, cos, sin, wq, wk, wv, out_0, out_1, 
                 stop=True,
             )
 
-        def project_head(step, head, out):
-            x_codes, x_scales = step["group"]["codes"]
-            n = step["group"]["tiles"]
+        def project_head(unit, head, out):
+            x_codes, x_scales = unit["group"]["codes"]
+            n = unit["group"]["tiles"]
             columns = slice(head * HD, (head + 1) * HD)
             nc.tensor.matmul_mx(
                 out=out,
@@ -228,193 +228,188 @@ def tile_titanstnt_pa_t_kernel(tc, x, pmem, cos, sin, wq, wk, wv, out_0, out_1, 
                 stop=True,
             )
 
-        def start_k(step):
-            n = step["group"]["tiles"]
-            step["k_banks"] = []
-            if n == 1:
-                acc = psum.tile([P, GROUP * P], F32, name="kacc")
+        def start_k(unit):
+            acc = psum.tile([P, GROUP * P], F32, name="k_bank")
+            if unit["group"]["tiles"] == 1:
                 for head in range(H):
-                    project_head(step, head, acc[:, head * P : (head + 1) * P])
-                step["k_banks"].append(acc)
+                    project_head(unit, head, acc[:, head * P : (head + 1) * P])
             else:
-                for j in range(STEP):
-                    acc = psum.tile([P, GROUP * P], F32, name="kacc")
-                    project_head(step, step["half"] * STEP + j, acc[:])
-                    step["k_banks"].append(acc)
+                project_head(unit, unit["part"], acc[:])
+            unit["k_bank"] = acc
+            unit["k_parts"] = kparts.tile([P, 2, GROUP * P], F32, name="k_parts")
 
-        def on_gpsimd(step, j):
-            return step["group"]["tiles"] > 1 and step["half"] == 1 and j == 1
+        def gpsimd_rows(unit):
+            return GPSIMD_ROWS[unit["part"]] if unit["group"]["tiles"] > 1 else ()
 
-        def copy_k_for_gpsimd(step):
-            for j, acc in enumerate(step["k_banks"]):
-                if on_gpsimd(step, j):
-                    k_copy = stage.tile([P, GROUP * P], F32)
-                    nc.scalar.copy(out=k_copy[:], in_=acc[:])
-                    step["k_copy"] = k_copy
+        def multiply_k(unit, source, rows, engine):
+            n, slot = unit["group"]["tiles"], unit["group"]["slot"]
+            if not rows:
+                return
+            m = len(rows)
+            rows = slice(rows[0], rows[-1] + 1)
+            parts = unit["k_parts"][:, rows]
+            values = tables_t[:, rows, slot * P : (slot + n) * P]
+            if n == 1:
+                engine.tensor_tensor(
+                    out=parts.rearrange("p w (h r) -> p w h r", h=H),
+                    in0=source[:].rearrange("p (h r) -> p h r", h=H).unsqueeze(1).to_broadcast([P, m, H, P]),
+                    in1=values.unsqueeze(2).to_broadcast([P, m, H, P]),
+                    op=MULT,
+                )
+            else:
+                engine.tensor_tensor(
+                    out=parts, in0=source[:].unsqueeze(1).to_broadcast([P, m, GROUP * P]), in1=values, op=MULT
+                )
 
-        def multiply_k(step, gpsimd):
-            n, slot = step["group"]["tiles"], step["group"]["slot"]
-            columns = slice(slot * P, (slot + n) * P)
-            if "k_parts" not in step:
-                step["k_parts"] = [None for acc in step["k_banks"]]
-            for j, acc in enumerate(step["k_banks"]):
-                if on_gpsimd(step, j) != gpsimd:
-                    continue
-                by_cos_t = kparts.tile([P, GROUP * P], F32)
-                by_sin_t = kparts.tile([P, GROUP * P], F32)
-                source = step["k_copy"] if gpsimd else acc
-                engine = nc.gpsimd if gpsimd else nc.vector
-                for part, table in ((by_cos_t, cos_t), (by_sin_t, sin_t)):
-                    values = table[:, columns]
-                    if n == 1:
-                        engine.tensor_tensor(
-                            out=part[:].rearrange("p (h r) -> p h r", h=H),
-                            in0=source[:].rearrange("p (h r) -> p h r", h=H),
-                            in1=values.unsqueeze(1).to_broadcast([P, H, P]),
-                            op=MULT,
-                        )
-                    else:
-                        engine.tensor_tensor(out=part[:], in0=source[:], in1=values, op=MULT)
-                step["k_parts"][j] = (by_cos_t, by_sin_t)
+        def multiply_k_on_vector(unit):
+            rows = [row for row in range(2) if row not in gpsimd_rows(unit)]
+            multiply_k(unit, unit["k_bank"], rows, nc.vector)
 
-        def add_k(step):
-            group = step["group"]
-            if step["half"] == 0:
+        def multiply_k_on_gpsimd(unit):
+            rows = gpsimd_rows(unit)
+            if rows:
+                k_copy = stage.tile([P, GROUP * P], F32)
+                nc.scalar.copy(out=k_copy[:], in_=unit["k_bank"][:])
+                multiply_k(unit, k_copy, rows, nc.gpsimd)
+
+        def add_k(unit):
+            group = unit["group"]
+            if unit["part"] == 0:
                 group["k_sb"] = kresults.tile([P, GROUP, D], F32, name="k_sb")
-            for j, (by_cos_t, by_sin_t) in enumerate(step["k_parts"]):
-                ko = psum.tile([P, GROUP, P], F32)
-                for i in range(GROUP):
-                    columns = slice(i * P, (i + 1) * P)
+            ko = psum.tile([P, GROUP, P], F32)
+            for i in range(GROUP):
+                columns = slice(i * P, (i + 1) * P)
+                for row, matrix in ((0, identity), (1, swap)):
                     nc.tensor.matmul(
-                        ko[:, i, :], lhsT=by_cos_t[:, columns], rhs=identity[:], start=True, stop=False, is_transpose=True
+                        ko[:, i, :],
+                        lhsT=unit["k_parts"][:, row, columns],
+                        rhs=matrix[:],
+                        start=row == 0,
+                        stop=row == 1,
+                        is_transpose=True,
                     )
-                    nc.tensor.matmul(
-                        ko[:, i, :], lhsT=by_sin_t[:, columns], rhs=swap[:], start=False, stop=True, is_transpose=True
-                    )
-                if group["tiles"] == 1:
-                    nc.scalar.copy(out=group["k_sb"][:, 0, :].rearrange("p (h d) -> p h d", h=H), in_=ko[:])
-                else:
-                    head = step["half"] * STEP + j
-                    nc.scalar.copy(out=group["k_sb"][:, :, head * HD : (head + 1) * HD], in_=ko[:])
+            if group["tiles"] == 1:
+                nc.scalar.copy(out=group["k_sb"][:, 0, :].rearrange("p (h d) -> p h d", h=H), in_=ko[:])
+            else:
+                nc.scalar.copy(out=group["k_sb"][:, :, unit["part"] * HD : (unit["part"] + 1) * HD], in_=ko[:])
 
-        def start_q(step):
-            step["q_banks"] = []
-            for i in range(step["tiles"]):
-                acc = psum.tile([P, D], F32, name="qacc")
-                project(step, step["half"] * STEP + i, Q, acc)
-                step["q_banks"].append(acc)
+        def start_q(unit):
+            acc = psum.tile([P, D], F32, name="q_bank")
+            project(unit, Q, acc)
+            unit["q_bank"] = acc
 
-        def multiply_q(step, i):
+        def multiply_q(unit):
+            i = unit["part"] % PAIR
             if i == 0:
-                by_cos = results.tile([P, STEP, D], F32)
-                by_sin = results.tile([P, STEP, D], F32)
-                step["q_parts"] = (by_cos, by_sin)
-            by_cos, by_sin = step["q_parts"]
-            if i < step["tiles"]:
-                acc = step["q_banks"][i]
-                slot = step["group"]["slot"] + step["half"] * STEP + i
-                for part, table in ((by_cos, cos_sb), (by_sin, sin_sb)):
-                    nc.vector.tensor_tensor(
-                        out=part[:, i, :].rearrange("p (h d) -> p h d", h=H),
-                        in0=acc[:].rearrange("p (h d) -> p h d", h=H),
-                        in1=table[:, slot, :].unsqueeze(1).to_broadcast([P, H, HD]),
-                        op=MULT,
-                    )
+                unit["group"]["q_parts"] = results.tile([P, 2, PAIR, D], F32, name="q_parts")
+            slot = unit["group"]["slot"] + unit["part"]
+            nc.vector.tensor_tensor(
+                out=unit["group"]["q_parts"][:, :, i, :].rearrange("p w (h d) -> p w h d", h=H),
+                in0=unit["q_bank"][:].rearrange("p (h d) -> p h d", h=H).unsqueeze(1).to_broadcast([P, 2, H, HD]),
+                in1=tables[:, :, slot, :].unsqueeze(2).to_broadcast([P, 2, H, HD]),
+                op=MULT,
+            )
 
-        def add_q(step, engine):
-            n = step["tiles"]
-            by_cos, by_sin = step["q_parts"]
-            cos_halves = by_cos[:, 0:n, :].rearrange("p i (h s d) -> p i h s d", h=H, s=2)
-            sin_halves = by_sin[:, 0:n, :].rearrange("p i (h s d) -> p i h s d", h=H, s=2)
+        def add_q(unit, engine, m):
+            i1 = unit["part"] % PAIR + 1
+            q_parts = unit["group"]["q_parts"]
+            cos_halves = q_parts[:, 0, i1 - m : i1, :].rearrange("p i (h s d) -> p i h s d", h=H, s=2)
+            sin_halves = q_parts[:, 1, i1 - m : i1, :].rearrange("p i (h s d) -> p i h s d", h=H, s=2)
             for s in range(2):
                 engine.tensor_tensor(
                     out=cos_halves[:, :, :, s, :], in0=cos_halves[:, :, :, s, :], in1=sin_halves[:, :, :, 1 - s, :], op=ADD
                 )
+            store(unit, out_0, q_parts[:, 0, i1 - m : i1, :], m)
 
-        def store(group, out, result, i0, m):
+        def project_v(unit):
+            i = unit["part"] % PAIR
+            if i == 0:
+                unit["group"]["v_sb"] = results.tile([P, PAIR, D], F32, name="v_sb")
+            acc = psum.tile([P, D], F32, name="misc")
+            project(unit, V, acc)
+            nc.scalar.copy(out=unit["group"]["v_sb"][:, i, :], in_=acc[:])
+
+        def store(unit, out, result, m):
+            group, n = unit["group"], unit["group"]["tiles"]
+            i1 = unit["part"] + 1
+            for b, row in group["stores"]:
+                nc.sync.dma_start(
+                    out=out[b, row : row + n * P].rearrange("(p j) h d -> p j (h d)", j=n)[:, i1 - m : i1, :],
+                    in_=result,
+                )
+
+        def store_heads(group, h0, h1):
             n = group["tiles"]
             for b, row in group["stores"]:
                 nc.sync.dma_start(
-                    out=out[b, row : row + n * P].rearrange("(p j) h d -> p j (h d)", j=n)[:, i0 : i0 + m, :],
-                    in_=result[:, 0:m, :],
+                    out=out_1[b, row : row + n * P].rearrange("(p j) h d -> p j (h d)", j=n)[:, :, h0 * HD : h1 * HD],
+                    in_=group["k_sb"][:, 0:n, h0 * HD : h1 * HD],
                 )
 
-        def project_v(step, i):
-            if i == 0:
-                step["v_sb"] = results.tile([P, STEP, D], F32, name="v_sb")
-            acc = psum.tile([P, D], F32, name="misc")
-            project(step, step["half"] * STEP + i, V, acc)
-            nc.scalar.copy(out=step["v_sb"][:, i, :], in_=acc[:])
-
-        groups[0]["grouped"] = new_grouped()
-        transpose_tokens(groups[0], groups[0]["grouped"], 0, 1)
-        prepare_tables(groups[0])
+        first, begin = groups[0], units[0]
+        transpose_tokens(first, 0)
+        prepare_tables(first)
         group_weight(Q)
-        groups[0]["codes"] = quantise_tokens(groups[0], groups[0]["grouped"])
+        quantise_tokens(first)
         quantise_weights(Q)
-        start_q(steps[0])
-        transpose_tables(groups[0])
+        start_q(begin)
         group_weight(K)
+        transpose_tables(first)
         quantise_weights(K)
-        start_k(steps[0])
-        multiply_q(steps[0], 0)
+        start_k(begin)
+        multiply_q(begin)
         group_weight(V)
-        groups[1]["grouped"] = new_grouped()
-        transpose_tokens(groups[1], groups[1]["grouped"], 0, STEP)
-        transpose_tokens(groups[1], groups[1]["grouped"], STEP, STEP)
+        for i in range(GROUP):
+            transpose_tokens(groups[1], i)
         prepare_tables(groups[1])
         transpose_tables(groups[1])
-        multiply_k(steps[0], gpsimd=False)
-        groups[1]["codes"] = quantise_tokens(groups[1], groups[1]["grouped"])
-        start_k(steps[1])
-        copy_k_for_gpsimd(steps[1])
+        multiply_k_on_vector(begin)
+        add_q(begin, nc.gpsimd, 1)
+        quantise_tokens(groups[1])
+        start_k(units[1])
+        start_q(units[1])
         quantise_weights(V)
-        multiply_k(steps[1], gpsimd=True)
-        add_q(steps[0], nc.gpsimd)
-        project_v(steps[0], 0)
-        groups[2]["grouped"] = new_grouped()
-        transpose_tokens(groups[2], groups[2]["grouped"], 0, STEP)
+        project_v(begin)
+        store(begin, out_2, first["v_sb"][:, 0:1, :], 1)
         prepare_tables(groups[2])
-        store(groups[0], out_2, steps[0]["v_sb"], 0, 1)
-        store(groups[0], out_0, steps[0]["q_parts"][0], 0, 1)
+        for i in range(PAIR):
+            transpose_tokens(groups[2], i)
 
-        for number, step in enumerate(steps):
-            if number == 0:
-                continue
-            group = step["group"]
-            before = steps[number - 1]
-            following = steps[number + 1] if number + 1 < len(steps) else None
-            next_group = groups[step["index"] + 1] if step["index"] + 1 < len(groups) else None
-            second_group = groups[step["index"] + 2] if step["index"] + 2 < len(groups) else None
-            second = step["half"] == 1
+        for number in range(1, len(units)):
+            unit, before = units[number], units[number - 1]
+            following = units[number + 1] if number + 1 < len(units) else None
+            group, part = unit["group"], unit["part"]
+            next_group = groups[unit["index"] + 1] if unit["index"] + 1 < len(groups) else None
+            second_group = groups[unit["index"] + 2] if unit["index"] + 2 < len(groups) else None
+            last_group = next_group is None
 
-            multiply_k(step, gpsimd=False)
-            start_q(step)
-            multiply_q(step, 0)
-            if second and next_group is not None:
-                next_group["codes"] = quantise_tokens(next_group, next_group["grouped"])
-            add_k(before)
-            if before["half"] == 1 or number == 1:
-                store(before["group"], out_1, before["group"]["k_sb"], 0, before["group"]["tiles"])
-            if not second and next_group is not None:
-                transpose_tokens(next_group, next_group["grouped"], STEP, STEP)
-            if second and second_group is not None:
-                second_group["grouped"] = new_grouped()
-                transpose_tokens(second_group, second_group["grouped"], 0, STEP)
-            if next_group is not None and next_group["loads_tables"] and not second:
-                transpose_tables(next_group)
+            multiply_k_on_vector(unit)
+            if part == 2 and next_group is not None:
+                quantise_tokens(next_group)
             if following is not None:
                 start_k(following)
-                copy_k_for_gpsimd(following)
-            if second and second_group is not None and second_group["loads_tables"]:
+                start_q(following)
+                multiply_k_on_gpsimd(following)
+            project_v(unit)
+            if part % PAIR == PAIR - 1:
+                store(unit, out_2, group["v_sb"][:], PAIR)
+            multiply_q(unit)
+            add_k(before)
+            if before["part"] == before["group"]["tiles"] - 1:
+                store_heads(before["group"], 0, H)
+            if part < PAIR and next_group is not None:
+                transpose_tokens(next_group, part + PAIR)
+            if part >= PAIR and second_group is not None:
+                transpose_tokens(second_group, part - PAIR)
+            if part == 1 and next_group is not None and next_group["loads_tables"]:
+                transpose_tables(next_group)
+            if part == 2 and second_group is not None and second_group["loads_tables"]:
                 prepare_tables(second_group)
-            if following is not None:
-                multiply_k(following, gpsimd=True)
-            project_v(step, 0)
-            project_v(step, 1)
-            multiply_q(step, 1)
-            add_q(step, nc.gpsimd if following is not None else nc.vector)
-            store(group, out_2, step["v_sb"], step["half"] * STEP, step["tiles"])
-            store(group, out_0, step["q_parts"][0], step["half"] * STEP, step["tiles"])
-        add_k(steps[-1])
-        store(groups[-1], out_1, groups[-1]["k_sb"], 0, GROUP)
+            if last_group and part == 2:
+                store_heads(group, 0, PAIR)
+            if last_group:
+                add_q(unit, nc.vector if following is None else nc.gpsimd, 1)
+            elif part % PAIR == PAIR - 1:
+                add_q(unit, nc.gpsimd, PAIR)
+        add_k(units[-1])
+        store_heads(groups[-1], PAIR, H)

@@ -25,6 +25,7 @@ GROUPS_PER_SEQ = L // GROUP_TOKENS
 TABLE_SLOTS = GROUPS_PER_SEQ * GROUP + 1
 TOKEN_TILES = B * GROUPS_PER_SEQ * GROUP + 1
 WORDS = D // 2
+ROW = D + HD
 PAIR = 2
 Q, K, V = 0, 1, 2
 VECTOR_COLUMNS = 320
@@ -298,28 +299,37 @@ def tile_titanstnt_pa_t_kernel(tc, x, pmem, cos, sin, wq, wk, wv, out_0, out_1, 
             project(unit, Q, acc)
             unit["q_bank"] = acc
 
+        def products_of_half(parts, i, s):
+            start = i * 2 * ROW + s * HALF
+            step = ROW + HALF * (1 - 2 * s)
+            both = parts[:, start : start + 2 * step].rearrange("p (w c) -> p w c", w=2)
+            return both[:, :, 0:D].rearrange("p w (h d) -> p w h d", h=H)[:, :, :, 0:HALF]
+
         def multiply_q(unit):
             i = unit["part"] % PAIR
             if i == 0:
-                unit["group"]["q_parts"] = results.tile([P, 2, PAIR, D], F32, name="q_parts")
+                unit["group"]["q_parts"] = results.tile([P, PAIR * 2 * ROW + HD], F32, name="q_parts")
             slot = unit["group"]["slot"] + unit["part"]
-            nc.vector.tensor_tensor(
-                out=unit["group"]["q_parts"][:, :, i, :].rearrange("p w (h d) -> p w h d", h=H),
-                in0=unit["q_bank"][:].rearrange("p (h d) -> p h d", h=H).unsqueeze(1).to_broadcast([P, 2, H, HD]),
-                in1=tables[:, :, slot, :].unsqueeze(2).to_broadcast([P, 2, H, HD]),
-                op=MULT,
-            )
+            halves = unit["q_bank"][:].rearrange("p (h s d) -> p h s d", h=H, s=2)
+            for s in range(2):
+                nc.vector.tensor_tensor(
+                    out=products_of_half(unit["group"]["q_parts"], i, s),
+                    in0=halves[:, :, s, :].unsqueeze(1).to_broadcast([P, 2, H, HALF]),
+                    in1=tables[:, :, slot, s * HALF : (s + 1) * HALF].unsqueeze(2).to_broadcast([P, 2, H, HALF]),
+                    op=MULT,
+                )
 
         def add_q(unit, engine, m):
+            by_cos, by_sin = q_rows(unit, m)
+            engine.tensor_tensor(out=by_cos, in0=by_cos, in1=by_sin, op=ADD)
+
+        def q_rows(unit, m):
             i1 = unit["part"] % PAIR + 1
-            q_parts = unit["group"]["q_parts"]
-            cos_halves = q_parts[:, 0, i1 - m : i1, :].rearrange("p i (h s d) -> p i h s d", h=H, s=2)
-            sin_halves = q_parts[:, 1, i1 - m : i1, :].rearrange("p i (h s d) -> p i h s d", h=H, s=2)
-            for s in range(2):
-                engine.tensor_tensor(
-                    out=cos_halves[:, :, :, s, :], in0=cos_halves[:, :, :, s, :], in1=sin_halves[:, :, :, 1 - s, :], op=ADD
-                )
-            store(unit, out_0, q_parts[:, 0, i1 - m : i1, :], m)
+            rows = unit["group"]["q_parts"][:, 0 : PAIR * 2 * ROW].rearrange("p (i w c) -> p i w c", w=2, c=ROW)
+            return [rows[:, i1 - m : i1, w, 0:D] for w in range(2)]
+
+        def store_q(unit, m):
+            store(unit, out_0, q_rows(unit, m)[0], m)
 
         def project_v(unit):
             i = unit["part"] % PAIR
@@ -365,6 +375,7 @@ def tile_titanstnt_pa_t_kernel(tc, x, pmem, cos, sin, wq, wk, wv, out_0, out_1, 
         transpose_tables(groups[1])
         multiply_k_on_vector(begin)
         add_q(begin, nc.gpsimd, 1)
+        store_q(begin, 1)
         quantise_tokens(groups[1])
         start_k(units[1])
         start_q(units[1])
@@ -407,9 +418,8 @@ def tile_titanstnt_pa_t_kernel(tc, x, pmem, cos, sin, wq, wk, wv, out_0, out_1, 
                 prepare_tables(second_group)
             if last_group and part == 2:
                 store_heads(group, 0, PAIR)
-            if last_group:
-                add_q(unit, nc.vector if following is None else nc.gpsimd, 1)
-            elif part % PAIR == PAIR - 1:
-                add_q(unit, nc.gpsimd, PAIR)
+            add_q(unit, nc.vector if following is None else nc.gpsimd, 1)
+            if last_group or part % PAIR == PAIR - 1:
+                store_q(unit, 1 if last_group else PAIR)
         add_k(units[-1])
         store_heads(groups[-1], PAIR, H)

@@ -28,8 +28,8 @@ WORDS = D // 2
 ROW = D + HD
 PAIR = 2
 Q, K, V = 0, 1, 2
-VECTOR_COLUMNS = 320
-GPSIMD_ROWS = ((), (), (), (0, 1))
+GPSIMD_ROWS = ((), (1,), (), ())
+TURNED_HEADS = 3
 
 FLOPS = 2 * B * (L + P) * D * 3 * D
 
@@ -96,11 +96,8 @@ def tile_titanstnt_pa_t_kernel(tc, x, pmem, cos, sin, wq, wk, wv, out_0, out_1, 
         swap = keep.tile([P, P], F32)
         identity_bf = keep.tile([P, P], BF16)
 
-        def load_weight(index, w):
-            nc.sync.dma_start(
-                out=w_raw[:, index].rearrange("p t c -> p (t c)"),
-                in_=w.rearrange("(p t) c -> p (t c)", t=PACK),
-            )
+        def load_weight(index, w, columns=slice(0, D)):
+            nc.sync.dma_start(out=w_raw[:, index, :, columns], in_=w.rearrange("(p t) c -> p t c", t=PACK)[:, :, columns])
 
         def load_tokens(group):
             n = group["tiles"]
@@ -122,13 +119,14 @@ def tile_titanstnt_pa_t_kernel(tc, x, pmem, cos, sin, wq, wk, wv, out_0, out_1, 
                         ),
                     )
 
+        load_weight(Q, wq, slice(0, D // 2))
         load_tokens(groups[0])
-        load_weight(Q, wq)
+        load_weight(Q, wq, slice(D // 2, D))
         load_tables(groups[0])
         load_weight(K, wk)
-        load_weight(V, wv)
         load_tokens(groups[1])
         load_tables(groups[1])
+        load_weight(V, wv)
         for group in groups[2:]:
             load_tokens(group)
             load_tables(group)
@@ -138,16 +136,19 @@ def tile_titanstnt_pa_t_kernel(tc, x, pmem, cos, sin, wq, wk, wv, out_0, out_1, 
         nc.gpsimd.tensor_copy(out=swap[:, 0:HALF], in_=identity[:, HALF:HD])
         nc.gpsimd.tensor_copy(out=swap[:, HALF:HD], in_=identity[:, 0:HALF])
 
-        def transpose_tokens(group, i):
-            if i == 0:
+        def transpose_tokens(group, i0, m=1, bank="misc"):
+            if i0 == 0:
                 group["grouped"] = stage.tile([P, GROUP * P * PACK], BF16, align_bytes=64, name="grouped")
-            xt = psum.tile([P, 2, P], F32, name="misc")
-            for u in range(2):
-                start = (group["first_tile"] + i) * WORDS
-                nc.tensor.transpose(xt[:, u, :], x_words[:, start + u : start + WORDS : 2], identity[:])
+            xt = psum.tile([P, m, 2, P], F32, name=bank)
+            for i in range(m):
+                for u in range(2):
+                    start = (group["first_tile"] + i0 + i) * WORDS
+                    nc.tensor.transpose(xt[:, i, u, :], x_words[:, start + u : start + WORDS : 2], identity[:])
             nc.scalar.copy(
-                out=group["grouped"][:].bitcast(F32)[:, i * 2 * P : (i + 1) * 2 * P].rearrange("p (r u) -> p r u", u=2),
-                in_=xt[:].rearrange("p u r -> p r u"),
+                out=group["grouped"][:].bitcast(F32)[:, i0 * 2 * P : (i0 + m) * 2 * P].rearrange(
+                    "p (i r u) -> p i r u", i=m, u=2
+                ),
+                in_=xt[:].rearrange("p i u r -> p i r u"),
             )
 
         def quantise_tokens(group):
@@ -164,15 +165,8 @@ def tile_titanstnt_pa_t_kernel(tc, x, pmem, cos, sin, wq, wk, wv, out_0, out_1, 
         def prepare_tables(group):
             n, slot = group["tiles"], group["slot"]
             slots = slice(slot, slot + n)
-            for half, sign in ((0, 1.0), (1, -1.0)):
-                nc.gpsimd.tensor_scalar(
-                    out=tables[:, 1, slots, half * HALF : (half + 1) * HALF],
-                    in0=sin_raw[:, slots, (1 - half) * HALF : (2 - half) * HALF],
-                    scalar1=sign,
-                    scalar2=0.0,
-                    op0=MULT,
-                    op1=ADD,
-                )
+            nc.scalar.copy(out=tables[:, 1, slots, 0:HALF], in_=sin_raw[:, slots, HALF:HD])
+            nc.scalar.mul(out=tables[:, 1, slots, HALF:HD], in_=sin_raw[:, slots, 0:HALF], mul=-1.0)
 
         def transpose_tables(group):
             n, slot = group["tiles"], group["slot"]
@@ -185,15 +179,11 @@ def tile_titanstnt_pa_t_kernel(tc, x, pmem, cos, sin, wq, wk, wv, out_0, out_1, 
                 out=tables_t[:, :, columns].rearrange("p w (i r) -> p w i r", i=n), in_=tt[:, :, 0:n, :]
             )
 
-        def group_weight(index):
-            for columns, copy in (
-                (slice(0, VECTOR_COLUMNS), nc.vector.tensor_copy),
-                (slice(VECTOR_COLUMNS, D), nc.scalar.copy),
-            ):
-                copy(
-                    out=w_grouped[:, index, columns, :],
-                    in_=w_raw[:, index, :, columns].rearrange("p t c -> p c t"),
-                )
+        def group_weight(index, c0, c1, copy):
+            copy(
+                out=w_grouped[:, index, c0:c1, :],
+                in_=w_raw[:, index, :, c0:c1].rearrange("p t c -> p c t"),
+            )
 
         def quantise_weights(index):
             nc.vector.quantize_mx(
@@ -231,16 +221,33 @@ def tile_titanstnt_pa_t_kernel(tc, x, pmem, cos, sin, wq, wk, wv, out_0, out_1, 
 
         def start_k(unit):
             acc = psum.tile([P, GROUP * P], F32, name="k_bank")
+            unit["k_bank"] = acc
+            unit["straight"] = unit["part"] >= TURNED_HEADS
+            if unit["straight"]:
+                x_codes, x_scales = unit["group"]["codes"]
+                columns = slice(unit["part"] * HD, D)
+                for i in range(GROUP):
+                    tokens = slice(i * P, (i + 1) * P)
+                    nc.tensor.matmul_mx(
+                        out=acc[:, tokens],
+                        lhsT=x_codes[:, tokens].bitcast(FP8X4),
+                        lhsT_scale=x_scales[:, tokens],
+                        rhs=w_codes[:, K, columns].bitcast(FP8X4),
+                        rhs_scale=w_scales[:, K, columns],
+                        start=True,
+                        stop=True,
+                    )
+                unit["k_parts"] = stage.tile([P, 2 * ROW + HD], F32, name="straight")
+                return
             if unit["group"]["tiles"] == 1:
                 for head in range(H):
                     project_head(unit, head, acc[:, head * P : (head + 1) * P])
             else:
                 project_head(unit, unit["part"], acc[:])
-            unit["k_bank"] = acc
             unit["k_parts"] = kparts.tile([P, 2, GROUP * P], F32, name="k_parts")
 
         def gpsimd_rows(unit):
-            return GPSIMD_ROWS[unit["part"]] if unit["group"]["tiles"] > 1 else ()
+            return GPSIMD_ROWS[unit["part"]] if unit["group"]["tiles"] > 1 and not unit["straight"] else ()
 
         def multiply_k(unit, source, rows, engine):
             n, slot = unit["group"]["tiles"], unit["group"]["slot"]
@@ -262,7 +269,30 @@ def tile_titanstnt_pa_t_kernel(tc, x, pmem, cos, sin, wq, wk, wv, out_0, out_1, 
                     out=parts, in0=source[:].unsqueeze(1).to_broadcast([P, m, GROUP * P]), in1=values, op=MULT
                 )
 
+        def multiply_straight(unit):
+            slot = unit["group"]["slot"]
+            halves = unit["k_bank"][:].rearrange("p (i s d) -> p i s d", i=GROUP, s=2)
+            for s in range(2):
+                nc.vector.tensor_tensor(
+                    out=products_of_half(unit["k_parts"], 0, s),
+                    in0=halves[:, :, s, :].unsqueeze(1).to_broadcast([P, 2, GROUP, HALF]),
+                    in1=tables[:, :, slot : slot + GROUP, s * HALF : (s + 1) * HALF],
+                    op=MULT,
+                )
+
+        def add_straight(unit, engine):
+            by_cos, by_sin = (
+                unit["k_parts"][:, w * ROW : w * ROW + D].rearrange("p (i d) -> p i d", i=GROUP) for w in range(2)
+            )
+            part = unit["part"]
+            engine.tensor_tensor(
+                out=unit["group"]["k_sb"][:, :, part * HD : (part + 1) * HD], in0=by_cos, in1=by_sin, op=ADD
+            )
+
         def multiply_k_on_vector(unit):
+            if unit["straight"]:
+                multiply_straight(unit)
+                return
             rows = [row for row in range(2) if row not in gpsimd_rows(unit)]
             multiply_k(unit, unit["k_bank"], rows, nc.vector)
 
@@ -357,34 +387,32 @@ def tile_titanstnt_pa_t_kernel(tc, x, pmem, cos, sin, wq, wk, wv, out_0, out_1, 
                 )
 
         first, begin = groups[0], units[0]
+        group_weight(Q, 0, D // 2, nc.vector.tensor_copy)
         transpose_tokens(first, 0)
         prepare_tables(first)
-        group_weight(Q)
+        group_weight(Q, 256, 384, nc.vector.tensor_copy)
+        group_weight(Q, 384, D, nc.scalar.copy)
         quantise_tokens(first)
         quantise_weights(Q)
-        start_q(begin)
-        group_weight(K)
+        group_weight(K, 0, 256, nc.vector.tensor_copy)
+        group_weight(K, 256, D, nc.scalar.copy)
         transpose_tables(first)
+        start_q(begin)
+        multiply_q(begin)
+        prepare_tables(groups[1])
+        transpose_tokens(groups[1], 0, PAIR)
+        transpose_tokens(groups[1], PAIR, PAIR, "ko")
         quantise_weights(K)
         start_k(begin)
-        multiply_q(begin)
-        group_weight(V)
-        for i in range(GROUP):
-            transpose_tokens(groups[1], i)
-        prepare_tables(groups[1])
+        group_weight(V, 0, 320, nc.vector.tensor_copy)
+        group_weight(V, 320, D, nc.scalar.copy)
         transpose_tables(groups[1])
-        multiply_k_on_vector(begin)
-        add_q(begin, nc.gpsimd, 1)
-        store_q(begin, 1)
         quantise_tokens(groups[1])
         start_k(units[1])
         start_q(units[1])
+        multiply_k_on_vector(begin)
+        multiply_k_on_vector(units[1])
         quantise_weights(V)
-        project_v(begin)
-        store(begin, out_2, first["v_sb"][:, 0:1, :], 1)
-        prepare_tables(groups[2])
-        for i in range(PAIR):
-            transpose_tokens(groups[2], i)
 
         for number in range(1, len(units)):
             unit, before = units[number], units[number - 1]
@@ -394,21 +422,35 @@ def tile_titanstnt_pa_t_kernel(tc, x, pmem, cos, sin, wq, wk, wv, out_0, out_1, 
             second_group = groups[unit["index"] + 2] if unit["index"] + 2 < len(groups) else None
             last_group = next_group is None
 
-            multiply_k_on_vector(unit)
-            if part == 2 and next_group is not None:
-                quantise_tokens(next_group)
+            if number > 1:
+                multiply_k_on_vector(unit)
             if following is not None:
                 start_k(following)
                 start_q(following)
                 multiply_k_on_gpsimd(following)
+            if number == 1:
+                add_q(begin, nc.gpsimd, 1)
+                store_q(begin, 1)
+            if number == 1:
+                transpose_tokens(groups[2], 0, PAIR)
+                prepare_tables(groups[2])
+                project_v(begin)
+                store(begin, out_2, first["v_sb"][:, 0:1, :], 1)
             project_v(unit)
-            if part % PAIR == PAIR - 1:
+            if last_group:
+                store(unit, out_2, group["v_sb"][:, part % PAIR : part % PAIR + 1, :], 1)
+            elif part % PAIR == PAIR - 1:
                 store(unit, out_2, group["v_sb"][:], PAIR)
             multiply_q(unit)
-            add_k(before)
-            if before["part"] == before["group"]["tiles"] - 1:
-                store_heads(before["group"], 0, H)
-            if part < PAIR and next_group is not None:
+            if part == 2 and next_group is not None:
+                quantise_tokens(next_group)
+            if not before["straight"]:
+                add_k(before)
+            if number == 1:
+                store_heads(first, 0, H)
+            if number == 1:
+                transpose_tokens(groups[2], PAIR, PAIR)
+            elif number > 2 and part < PAIR and next_group is not None:
                 transpose_tokens(next_group, part + PAIR)
             if part >= PAIR and second_group is not None:
                 transpose_tokens(second_group, part - PAIR)
@@ -418,8 +460,9 @@ def tile_titanstnt_pa_t_kernel(tc, x, pmem, cos, sin, wq, wk, wv, out_0, out_1, 
                 prepare_tables(second_group)
             if last_group and part == 2:
                 store_heads(group, 0, PAIR)
+            if unit["straight"]:
+                add_straight(unit, nc.gpsimd)
+                store_heads(group, PAIR if last_group else 0, H)
             add_q(unit, nc.vector if following is None else nc.gpsimd, 1)
             if last_group or part % PAIR == PAIR - 1:
                 store_q(unit, 1 if last_group else PAIR)
-        add_k(units[-1])
-        store_heads(groups[-1], PAIR, H)

@@ -28,8 +28,10 @@ WORDS = D // 2
 ROW = D + HD
 PAIR = 2
 Q, K, V = 0, 1, 2
-GPSIMD_ROWS = ((), (1,), (), ())
-TURNED_HEADS = 3
+GPSIMD_COLUMNS = (256, 512, 256, 0)
+LAST_GPSIMD_COLUMNS = (256, 512, 256, 0)
+TURNED_TILES = (4, 4, 4, 2)
+LAST_TURNED_TILES = (4, 4, 4, 4)
 
 FLOPS = 2 * B * (L + P) * D * 3 * D
 
@@ -205,9 +207,8 @@ def tile_titanstnt_pa_t_kernel(tc, x, pmem, cos, sin, wq, wk, wv, out_0, out_1, 
                 stop=True,
             )
 
-        def project_head(unit, head, out):
+        def project_head(unit, head, n, out):
             x_codes, x_scales = unit["group"]["codes"]
-            n = unit["group"]["tiles"]
             columns = slice(head * HD, (head + 1) * HD)
             nc.tensor.matmul_mx(
                 out=out,
@@ -219,96 +220,97 @@ def tile_titanstnt_pa_t_kernel(tc, x, pmem, cos, sin, wq, wk, wv, out_0, out_1, 
                 stop=True,
             )
 
+        def turned_tiles(unit):
+            if unit["group"]["tiles"] == 1:
+                return GROUP
+            return (LAST_TURNED_TILES if unit["group"] is groups[-1] else TURNED_TILES)[unit["part"]]
+
+        def gpsimd_columns(unit):
+            if unit["group"]["tiles"] == 1:
+                return 0
+            return (LAST_GPSIMD_COLUMNS if unit["group"] is groups[-1] else GPSIMD_COLUMNS)[unit["part"]]
+
         def start_k(unit):
             acc = psum.tile([P, GROUP * P], F32, name="k_bank")
             unit["k_bank"] = acc
-            unit["straight"] = unit["part"] >= TURNED_HEADS
-            if unit["straight"]:
-                x_codes, x_scales = unit["group"]["codes"]
-                columns = slice(unit["part"] * HD, D)
-                for i in range(GROUP):
+            x_codes, x_scales = unit["group"]["codes"]
+            turned = turned_tiles(unit)
+            if unit["group"]["tiles"] == 1:
+                for head in range(H):
+                    project_head(unit, head, 1, acc[:, head * P : (head + 1) * P])
+            elif turned > 0:
+                project_head(unit, unit["part"], turned, acc[:, 0 : turned * P])
+            if turned > 0:
+                unit["k_parts"] = kparts.tile([P, 2, GROUP * P], F32, name="k_parts")
+            if turned < GROUP:
+                head = slice(unit["part"] * HD, (unit["part"] + 1) * HD)
+                for i in range(turned, GROUP):
                     tokens = slice(i * P, (i + 1) * P)
                     nc.tensor.matmul_mx(
                         out=acc[:, tokens],
                         lhsT=x_codes[:, tokens].bitcast(FP8X4),
                         lhsT_scale=x_scales[:, tokens],
-                        rhs=w_codes[:, K, columns].bitcast(FP8X4),
-                        rhs_scale=w_scales[:, K, columns],
+                        rhs=w_codes[:, K, head].bitcast(FP8X4),
+                        rhs_scale=w_scales[:, K, head],
                         start=True,
                         stop=True,
                     )
-                unit["k_parts"] = stage.tile([P, 2 * ROW + HD], F32, name="straight")
-                return
+                unit["straight"] = stage.tile([P, 2 * ROW + HD], F32, name="straight")
+
+        def multiply_turned(unit, source, rows, c0, c1, engine):
+            slot, m = unit["group"]["slot"], rows.stop - rows.start
+            out = unit["k_parts"][:, rows, c0:c1]
             if unit["group"]["tiles"] == 1:
-                for head in range(H):
-                    project_head(unit, head, acc[:, head * P : (head + 1) * P])
-            else:
-                project_head(unit, unit["part"], acc[:])
-            unit["k_parts"] = kparts.tile([P, 2, GROUP * P], F32, name="k_parts")
-
-        def gpsimd_rows(unit):
-            return GPSIMD_ROWS[unit["part"]] if unit["group"]["tiles"] > 1 and not unit["straight"] else ()
-
-        def multiply_k(unit, source, rows, engine):
-            n, slot = unit["group"]["tiles"], unit["group"]["slot"]
-            if not rows:
-                return
-            m = len(rows)
-            rows = slice(rows[0], rows[-1] + 1)
-            parts = unit["k_parts"][:, rows]
-            values = tables_t[:, rows, slot * P : (slot + n) * P]
-            if n == 1:
                 engine.tensor_tensor(
-                    out=parts.rearrange("p w (h r) -> p w h r", h=H),
-                    in0=source[:].rearrange("p (h r) -> p h r", h=H).unsqueeze(1).to_broadcast([P, m, H, P]),
-                    in1=values.unsqueeze(2).to_broadcast([P, m, H, P]),
+                    out=out.rearrange("p w (h r) -> p w h r", h=H),
+                    in0=source.rearrange("p (h r) -> p h r", h=H).unsqueeze(1).to_broadcast([P, m, H, P]),
+                    in1=tables_t[:, rows, slot * P : (slot + 1) * P].unsqueeze(2).to_broadcast([P, m, H, P]),
                     op=MULT,
                 )
             else:
                 engine.tensor_tensor(
-                    out=parts, in0=source[:].unsqueeze(1).to_broadcast([P, m, GROUP * P]), in1=values, op=MULT
-                )
-
-        def multiply_straight(unit):
-            slot = unit["group"]["slot"]
-            halves = unit["k_bank"][:].rearrange("p (i s d) -> p i s d", i=GROUP, s=2)
-            for s in range(2):
-                nc.vector.tensor_tensor(
-                    out=products_of_half(unit["k_parts"], 0, s),
-                    in0=halves[:, :, s, :].unsqueeze(1).to_broadcast([P, 2, GROUP, HALF]),
-                    in1=tables[:, :, slot : slot + GROUP, s * HALF : (s + 1) * HALF],
+                    out=out,
+                    in0=source.unsqueeze(1).to_broadcast([P, m, c1 - c0]),
+                    in1=tables_t[:, rows, slot * P + c0 : slot * P + c1],
                     op=MULT,
                 )
-
-        def add_straight(unit, engine):
-            by_cos, by_sin = (
-                unit["k_parts"][:, w * ROW : w * ROW + D].rearrange("p (i d) -> p i d", i=GROUP) for w in range(2)
-            )
-            part = unit["part"]
-            engine.tensor_tensor(
-                out=unit["group"]["k_sb"][:, :, part * HD : (part + 1) * HD], in0=by_cos, in1=by_sin, op=ADD
-            )
 
         def multiply_k_on_vector(unit):
-            if unit["straight"]:
-                multiply_straight(unit)
-                return
-            rows = [row for row in range(2) if row not in gpsimd_rows(unit)]
-            multiply_k(unit, unit["k_bank"], rows, nc.vector)
+            acc, end = unit["k_bank"], turned_tiles(unit) * P
+            split = end - gpsimd_columns(unit)
+            if split > 0:
+                multiply_turned(unit, acc[:, 0:split], slice(0, 2), 0, split, nc.vector)
+            if split < end:
+                multiply_turned(unit, acc[:, split:end], slice(0, 1), split, end, nc.vector)
+            if end < GROUP * P:
+                turned = turned_tiles(unit)
+                n = GROUP - turned
+                slots = slice(unit["group"]["slot"] + turned, unit["group"]["slot"] + GROUP)
+                halves = acc[:, end:].rearrange("p (i s d) -> p i s d", i=n, s=2)
+                for s in range(2):
+                    nc.vector.tensor_tensor(
+                        out=products_of_half(unit["straight"], n, s),
+                        in0=halves[:, :, s, :].unsqueeze(1).to_broadcast([P, 2, n, HALF]),
+                        in1=tables[:, :, slots, s * HALF : (s + 1) * HALF],
+                        op=MULT,
+                    )
 
         def multiply_k_on_gpsimd(unit):
-            rows = gpsimd_rows(unit)
-            if rows:
+            end = turned_tiles(unit) * P
+            split = end - gpsimd_columns(unit)
+            if split < end:
                 k_copy = stage.tile([P, GROUP * P], F32)
-                nc.scalar.copy(out=k_copy[:], in_=unit["k_bank"][:])
-                multiply_k(unit, k_copy, rows, nc.gpsimd)
+                nc.scalar.copy(out=k_copy[:, 0 : end - split], in_=unit["k_bank"][:, split:end])
+                multiply_turned(unit, k_copy[:, 0 : end - split], slice(1, 2), split, end, nc.gpsimd)
 
-        def add_k(unit):
-            group = unit["group"]
+        def add_turned(unit):
+            group, turned = unit["group"], turned_tiles(unit)
             if unit["part"] == 0:
                 group["k_sb"] = kresults.tile([P, GROUP, D], F32, name="k_sb")
-            ko = psum.tile([P, GROUP, P], F32)
-            for i in range(GROUP):
+            if turned == 0:
+                return
+            ko = psum.tile([P, turned, P], F32, name="ko")
+            for i in range(turned):
                 columns = slice(i * P, (i + 1) * P)
                 for row, matrix in ((0, identity), (1, swap)):
                     nc.tensor.matmul(
@@ -322,18 +324,30 @@ def tile_titanstnt_pa_t_kernel(tc, x, pmem, cos, sin, wq, wk, wv, out_0, out_1, 
             if group["tiles"] == 1:
                 nc.scalar.copy(out=group["k_sb"][:, 0, :].rearrange("p (h d) -> p h d", h=H), in_=ko[:])
             else:
-                nc.scalar.copy(out=group["k_sb"][:, :, unit["part"] * HD : (unit["part"] + 1) * HD], in_=ko[:])
+                head = slice(unit["part"] * HD, (unit["part"] + 1) * HD)
+                nc.scalar.copy(out=group["k_sb"][:, 0:turned, head], in_=ko[:])
+
+        def add_straight(unit):
+            turned, part = turned_tiles(unit), unit["part"]
+            if turned < GROUP:
+                n = GROUP - turned
+                by_cos, by_sin = (
+                    unit["straight"][:, w * ROW : w * ROW + n * HD].rearrange("p (i d) -> p i d", i=n) for w in range(2)
+                )
+                nc.gpsimd.tensor_tensor(
+                    out=unit["group"]["k_sb"][:, turned:, part * HD : (part + 1) * HD], in0=by_cos, in1=by_sin, op=ADD
+                )
+
+        def products_of_half(parts, n, s):
+            start = s * HALF
+            step = ROW + HALF * (1 - 2 * s)
+            both = parts[:, start : start + 2 * step].rearrange("p (w c) -> p w c", w=2)
+            return both[:, :, 0 : n * HD].rearrange("p w (h d) -> p w h d", h=n)[:, :, :, 0:HALF]
 
         def start_q(unit):
             acc = psum.tile([P, D], F32, name="q_bank")
             project(unit, Q, acc)
             unit["q_bank"] = acc
-
-        def products_of_half(parts, i, s):
-            start = i * 2 * ROW + s * HALF
-            step = ROW + HALF * (1 - 2 * s)
-            both = parts[:, start : start + 2 * step].rearrange("p (w c) -> p w c", w=2)
-            return both[:, :, 0:D].rearrange("p w (h d) -> p w h d", h=H)[:, :, :, 0:HALF]
 
         def multiply_q(unit):
             i = unit["part"] % PAIR
@@ -343,7 +357,7 @@ def tile_titanstnt_pa_t_kernel(tc, x, pmem, cos, sin, wq, wk, wv, out_0, out_1, 
             halves = unit["q_bank"][:].rearrange("p (h s d) -> p h s d", h=H, s=2)
             for s in range(2):
                 nc.vector.tensor_tensor(
-                    out=products_of_half(unit["group"]["q_parts"], i, s),
+                    out=products_of_half(unit["group"]["q_parts"][:, i * 2 * ROW :], H, s),
                     in0=halves[:, :, s, :].unsqueeze(1).to_broadcast([P, 2, H, HALF]),
                     in1=tables[:, :, slot, s * HALF : (s + 1) * HALF].unsqueeze(2).to_broadcast([P, 2, H, HALF]),
                     op=MULT,
@@ -410,6 +424,7 @@ def tile_titanstnt_pa_t_kernel(tc, x, pmem, cos, sin, wq, wk, wv, out_0, out_1, 
         quantise_tokens(groups[1])
         start_k(units[1])
         start_q(units[1])
+        multiply_k_on_gpsimd(units[1])
         multiply_k_on_vector(begin)
         multiply_k_on_vector(units[1])
         quantise_weights(V)
@@ -444,10 +459,11 @@ def tile_titanstnt_pa_t_kernel(tc, x, pmem, cos, sin, wq, wk, wv, out_0, out_1, 
             multiply_q(unit)
             if part == 2 and next_group is not None:
                 quantise_tokens(next_group)
-            if not before["straight"]:
-                add_k(before)
+            add_turned(before)
             if number == 1:
                 store_heads(first, 0, H)
+            elif before["part"] == GROUP - 1:
+                store_heads(before["group"], PAIR if before["group"] is groups[-2] else 0, H)
             if number == 1:
                 transpose_tokens(groups[2], PAIR, PAIR)
             elif number > 2 and part < PAIR and next_group is not None:
@@ -458,11 +474,13 @@ def tile_titanstnt_pa_t_kernel(tc, x, pmem, cos, sin, wq, wk, wv, out_0, out_1, 
                 transpose_tables(next_group)
             if part == 2 and second_group is not None and second_group["loads_tables"]:
                 prepare_tables(second_group)
-            if last_group and part == 2:
+            if part == PAIR and (last_group or group is groups[-2]):
                 store_heads(group, 0, PAIR)
-            if unit["straight"]:
-                add_straight(unit, nc.gpsimd)
-                store_heads(group, PAIR if last_group else 0, H)
+            if following is None:
+                store_heads(group, 2, 3)
+                add_turned(unit)
+                store_heads(group, 3, H)
+            add_straight(unit)
             add_q(unit, nc.vector if following is None else nc.gpsimd, 1)
             if last_group or part % PAIR == PAIR - 1:
                 store_q(unit, 1 if last_group else PAIR)

@@ -28,9 +28,9 @@ WORDS = D // 2
 ROW = D + HD
 PAIR = 2
 Q, K, V = 0, 1, 2
-GPSIMD_COLUMNS = (256, 512, 256, 0)
-LAST_GPSIMD_COLUMNS = (256, 512, 256, 0)
-TURNED_TILES = (4, 4, 4, 2)
+GPSIMD_COLUMNS = (256, 0, 0, 0)
+LAST_GPSIMD_COLUMNS = (256, 0, 0, 0)
+TURNED_TILES = (4, 4, 4, 4)
 LAST_TURNED_TILES = (4, 4, 4, 4)
 
 FLOPS = 2 * B * (L + P) * D * 3 * D
@@ -97,6 +97,7 @@ def tile_titanstnt_pa_t_kernel(tc, x, pmem, cos, sin, wq, wk, wv, out_0, out_1, 
         identity = keep.tile([P, P], F32)
         swap = keep.tile([P, P], F32)
         identity_bf = keep.tile([P, P], BF16)
+        zeros = keep.tile([P, D], BF16)
 
         def load_weight(index, w, columns=slice(0, D)):
             nc.sync.dma_start(out=w_raw[:, index, :, columns], in_=w.rearrange("(p t) c -> p t c", t=PACK)[:, :, columns])
@@ -280,8 +281,6 @@ def tile_titanstnt_pa_t_kernel(tc, x, pmem, cos, sin, wq, wk, wv, out_0, out_1, 
             split = end - gpsimd_columns(unit)
             if split > 0:
                 multiply_turned(unit, acc[:, 0:split], slice(0, 2), 0, split, nc.vector)
-            if split < end:
-                multiply_turned(unit, acc[:, split:end], slice(0, 1), split, end, nc.vector)
             if end < GROUP * P:
                 turned = turned_tiles(unit)
                 n = GROUP - turned
@@ -301,7 +300,7 @@ def tile_titanstnt_pa_t_kernel(tc, x, pmem, cos, sin, wq, wk, wv, out_0, out_1, 
             if split < end:
                 k_copy = stage.tile([P, GROUP * P], F32)
                 nc.scalar.copy(out=k_copy[:, 0 : end - split], in_=unit["k_bank"][:, split:end])
-                multiply_turned(unit, k_copy[:, 0 : end - split], slice(1, 2), split, end, nc.gpsimd)
+                multiply_turned(unit, k_copy[:, 0 : end - split], slice(0, 2), split, end, nc.gpsimd)
 
         def add_turned(unit):
             group, turned = unit["group"], turned_tiles(unit)
@@ -400,8 +399,15 @@ def tile_titanstnt_pa_t_kernel(tc, x, pmem, cos, sin, wq, wk, wv, out_0, out_1, 
                     in_=group["k_sb"][:, 0:n, h0 * HD : h1 * HD],
                 )
 
+        def keep_warm(count):
+            for repeat in range(count):
+                unused = psum.tile([P, D], F32, name="k_bank")
+                nc.tensor.matmul(unused[:], lhsT=zeros[:, 0:P], rhs=zeros[:], start=True, stop=True)
+
+        nc.vector.memset(zeros[:], 0.0)
         first, begin = groups[0], units[0]
         group_weight(Q, 0, D // 2, nc.vector.tensor_copy)
+        keep_warm(4)
         transpose_tokens(first, 0)
         prepare_tables(first)
         group_weight(Q, 256, 384, nc.vector.tensor_copy)
@@ -410,17 +416,21 @@ def tile_titanstnt_pa_t_kernel(tc, x, pmem, cos, sin, wq, wk, wv, out_0, out_1, 
         quantise_weights(Q)
         group_weight(K, 0, 256, nc.vector.tensor_copy)
         group_weight(K, 256, D, nc.scalar.copy)
+        keep_warm(2)
         transpose_tables(first)
+        keep_warm(2)
         start_q(begin)
         multiply_q(begin)
         prepare_tables(groups[1])
         transpose_tokens(groups[1], 0, PAIR)
         transpose_tokens(groups[1], PAIR, PAIR, "ko")
+        keep_warm(2)
         quantise_weights(K)
         start_k(begin)
         group_weight(V, 0, 320, nc.vector.tensor_copy)
         group_weight(V, 320, D, nc.scalar.copy)
         transpose_tables(groups[1])
+        keep_warm(2)
         quantise_tokens(groups[1])
         start_k(units[1])
         start_q(units[1])

@@ -30,7 +30,7 @@ PAIR = 2
 Q, K, V = 0, 1, 2
 GPSIMD_COLUMNS = (256, 0, 0, 0)
 LAST_GPSIMD_COLUMNS = (256, 0, 0, 0)
-TURNED_TILES = (4, 4, 4, 4)
+TURNED_TILES = (4, 2, 4, 4)
 LAST_TURNED_TILES = (4, 4, 4, 4)
 
 FLOPS = 2 * B * (L + P) * D * 3 * D

from contextlib import ExitStack

import concourse.mybir as mybir
from concourse.masks import make_identity

F32 = mybir.dt.float32
BF16 = mybir.dt.bfloat16
U32 = mybir.dt.uint32
U8 = mybir.dt.uint8
FP8X4 = mybir.dt.float8_e4m3fn_x4
MULT = mybir.AluOpType.mult
ADD = mybir.AluOpType.add

P = 128
PACK = 4
B = 2
L = 2048
D = 512
H = 4
HD = D // H
HALF = HD // 2
GROUP = 4
GROUP_TOKENS = GROUP * P
GROUPS_PER_SEQ = L // GROUP_TOKENS
TABLE_SLOTS = GROUPS_PER_SEQ * GROUP + 1
TOKEN_TILES = B * GROUPS_PER_SEQ * GROUP + 1
WORDS = D // 2
ROW = D + HD
PAIR = 2
Q, K, V = 0, 1, 2
GPSIMD_COLUMNS = (256, 0, 0, 0)
LAST_GPSIMD_COLUMNS = (256, 0, 0, 0)
TURNED_TILES = (4, 2, 4, 4)
LAST_TURNED_TILES = (4, 4, 4, 4)

FLOPS = 2 * B * (L + P) * D * 3 * D


def token_groups(x, pmem):
    groups = [
        {
            "rows": pmem[0],
            "tiles": 1,
            "slot": GROUPS_PER_SEQ * GROUP,
            "table_row": 0,
            "loads_tables": True,
            "stores": [(b, 0) for b in range(B)],
        }
    ]
    for b in range(B):
        for g in range(GROUPS_PER_SEQ):
            row = g * GROUP_TOKENS
            groups.append(
                {
                    "rows": x[b, row : row + GROUP_TOKENS, :],
                    "tiles": GROUP,
                    "slot": g * GROUP,
                    "table_row": P + row,
                    "loads_tables": b == 0,
                    "stores": [(b, P + row)],
                }
            )
    first_tile = 0
    for group in groups:
        group["first_tile"] = first_tile
        first_tile += group["tiles"]
    return groups


def tile_titanstnt_pa_t_kernel(tc, x, pmem, cos, sin, wq, wk, wv, out_0, out_1, out_2):
    nc = tc.nc
    groups = token_groups(x, pmem)
    units = [
        {"index": index, "group": group, "part": part}
        for index, group in enumerate(groups)
        for part in range(group["tiles"])
    ]

    with ExitStack() as ctx:
        keep = ctx.enter_context(tc.tile_pool(name="keep", bufs=1))
        stage = ctx.enter_context(tc.tile_pool(name="stage", bufs=2))
        kparts = ctx.enter_context(tc.tile_pool(name="kparts", bufs=4))
        results = ctx.enter_context(tc.tile_pool(name="results", bufs=5))
        kresults = ctx.enter_context(tc.tile_pool(name="kresults", bufs=3))
        psum = ctx.enter_context(tc.psum_pool(name="psum", bufs=2))
        ctx.enter_context(tc.manual_schedule())

        x_all = keep.tile([P, TOKEN_TILES * D], BF16)
        x_words = x_all[:].bitcast(F32)
        tables = keep.tile([P, 2, TABLE_SLOTS, HD], BF16)
        sin_raw = keep.tile([P, TABLE_SLOTS, HD], BF16)
        tables_t = keep.tile([P, 2, TABLE_SLOTS * P], BF16)
        w_raw = keep.tile([P, 3, PACK, D], BF16)
        w_grouped = keep.tile([P, 3, D, PACK], BF16, align_bytes=64)
        w_codes = keep.tile([P, 3, D], U32, align_bytes=64)
        w_scales = keep.tile([P, 3, D], U8, align_bytes=64)
        identity = keep.tile([P, P], F32)
        swap = keep.tile([P, P], F32)
        identity_bf = keep.tile([P, P], BF16)
        zeros = keep.tile([P, D], BF16)

        def load_weight(index, w, columns=slice(0, D)):
            nc.sync.dma_start(out=w_raw[:, index, :, columns], in_=w.rearrange("(p t) c -> p t c", t=PACK)[:, :, columns])

        def load_tokens(group):
            n = group["tiles"]
            start = group["first_tile"] * D
            nc.sync.dma_start(
                out=x_all[:, start : start + n * D],
                in_=group["rows"].rearrange("(p j) k -> p (j k)", j=n),
            )

        def load_tables(group):
            n = group["tiles"]
            if group["loads_tables"]:
                slots = slice(group["slot"], group["slot"] + n)
                for table_sb, table in ((tables[:, 0, slots, :], cos), (sin_raw[:, slots, :], sin)):
                    nc.sync.dma_start(
                        out=table_sb,
                        in_=table[group["table_row"] : group["table_row"] + n * P, :].rearrange(
                            "(p j) d -> p j d", j=n
                        ),
                    )

        load_weight(Q, wq, slice(0, D // 2))
        load_tokens(groups[0])
        load_weight(Q, wq, slice(D // 2, D))
        load_tables(groups[0])
        load_weight(K, wk)
        load_tokens(groups[1])
        load_tables(groups[1])
        load_weight(V, wv)
        for group in groups[2:]:
            load_tokens(group)
            load_tables(group)

        make_identity(nc, identity[:])
        make_identity(nc, identity_bf[:])
        nc.gpsimd.tensor_copy(out=swap[:, 0:HALF], in_=identity[:, HALF:HD])
        nc.gpsimd.tensor_copy(out=swap[:, HALF:HD], in_=identity[:, 0:HALF])

        def transpose_tokens(group, i0, m=1, bank="misc"):
            if i0 == 0:
                group["grouped"] = stage.tile([P, GROUP * P * PACK], BF16, align_bytes=64, name="grouped")
            xt = psum.tile([P, m, 2, P], F32, name=bank)
            for i in range(m):
                for u in range(2):
                    start = (group["first_tile"] + i0 + i) * WORDS
                    nc.tensor.transpose(xt[:, i, u, :], x_words[:, start + u : start + WORDS : 2], identity[:])
            nc.scalar.copy(
                out=group["grouped"][:].bitcast(F32)[:, i0 * 2 * P : (i0 + m) * 2 * P].rearrange(
                    "p (i r u) -> p i r u", i=m, u=2
                ),
                in_=xt[:].rearrange("p i u r -> p i r u"),
            )

        def quantise_tokens(group):
            n, grouped = group["tiles"], group["grouped"]
            x_codes = stage.tile([P, GROUP * P], U32, align_bytes=64)
            x_scales = stage.tile([P, GROUP * P], U8, align_bytes=64)
            nc.vector.quantize_mx(
                out=x_codes[:, : n * P].bitcast(FP8X4),
                scales=x_scales[:, : n * P],
                in_=grouped[:, : n * P * PACK],
            )
            group["codes"] = (x_codes, x_scales)

        def prepare_tables(group):
            n, slot = group["tiles"], group["slot"]
            slots = slice(slot, slot + n)
            nc.scalar.copy(out=tables[:, 1, slots, 0:HALF], in_=sin_raw[:, slots, HALF:HD])
            nc.scalar.mul(out=tables[:, 1, slots, HALF:HD], in_=sin_raw[:, slots, 0:HALF], mul=-1.0)

        def transpose_tables(group):
            n, slot = group["tiles"], group["slot"]
            tt = psum.tile([P, 2, GROUP, P], BF16, name="misc")
            for row in range(2):
                for i in range(n):
                    nc.tensor.transpose(tt[:, row, i, :], tables[:, row, slot + i, :], identity_bf[:])
            columns = slice(slot * P, (slot + n) * P)
            nc.scalar.copy(
                out=tables_t[:, :, columns].rearrange("p w (i r) -> p w i r", i=n), in_=tt[:, :, 0:n, :]
            )

        def group_weight(index, c0, c1, copy):
            copy(
                out=w_grouped[:, index, c0:c1, :],
                in_=w_raw[:, index, :, c0:c1].rearrange("p t c -> p c t"),
            )

        def quantise_weights(index):
            nc.vector.quantize_mx(
                out=w_codes[:, index].bitcast(FP8X4),
                scales=w_scales[:, index],
                in_=w_grouped[:, index].rearrange("p c t -> p (c t)"),
            )

        def project(unit, index, acc):
            x_codes, x_scales = unit["group"]["codes"]
            columns = slice(unit["part"] * P, (unit["part"] + 1) * P)
            nc.tensor.matmul_mx(
                out=acc[:],
                lhsT=x_codes[:, columns].bitcast(FP8X4),
                lhsT_scale=x_scales[:, columns],
                rhs=w_codes[:, index].bitcast(FP8X4),
                rhs_scale=w_scales[:, index],
                start=True,
                stop=True,
            )

        def project_head(unit, head, n, out):
            x_codes, x_scales = unit["group"]["codes"]
            columns = slice(head * HD, (head + 1) * HD)
            nc.tensor.matmul_mx(
                out=out,
                lhsT=w_codes[:, K, columns].bitcast(FP8X4),
                lhsT_scale=w_scales[:, K, columns],
                rhs=x_codes[:, : n * P].bitcast(FP8X4),
                rhs_scale=x_scales[:, : n * P],
                start=True,
                stop=True,
            )

        def turned_tiles(unit):
            if unit["group"]["tiles"] == 1:
                return GROUP
            return (LAST_TURNED_TILES if unit["group"] is groups[-1] else TURNED_TILES)[unit["part"]]

        def gpsimd_columns(unit):
            if unit["group"]["tiles"] == 1:
                return 0
            return (LAST_GPSIMD_COLUMNS if unit["group"] is groups[-1] else GPSIMD_COLUMNS)[unit["part"]]

        def start_k(unit):
            acc = psum.tile([P, GROUP * P], F32, name="k_bank")
            unit["k_bank"] = acc
            x_codes, x_scales = unit["group"]["codes"]
            turned = turned_tiles(unit)
            if unit["group"]["tiles"] == 1:
                for head in range(H):
                    project_head(unit, head, 1, acc[:, head * P : (head + 1) * P])
            elif turned > 0:
                project_head(unit, unit["part"], turned, acc[:, 0 : turned * P])
            if turned > 0:
                unit["k_parts"] = kparts.tile([P, 2, GROUP * P], F32, name="k_parts")
            if turned < GROUP:
                head = slice(unit["part"] * HD, (unit["part"] + 1) * HD)
                for i in range(turned, GROUP):
                    tokens = slice(i * P, (i + 1) * P)
                    nc.tensor.matmul_mx(
                        out=acc[:, tokens],
                        lhsT=x_codes[:, tokens].bitcast(FP8X4),
                        lhsT_scale=x_scales[:, tokens],
                        rhs=w_codes[:, K, head].bitcast(FP8X4),
                        rhs_scale=w_scales[:, K, head],
                        start=True,
                        stop=True,
                    )
                unit["straight"] = stage.tile([P, 2 * ROW + HD], F32, name="straight")

        def multiply_turned(unit, source, rows, c0, c1, engine):
            slot, m = unit["group"]["slot"], rows.stop - rows.start
            out = unit["k_parts"][:, rows, c0:c1]
            if unit["group"]["tiles"] == 1:
                engine.tensor_tensor(
                    out=out.rearrange("p w (h r) -> p w h r", h=H),
                    in0=source.rearrange("p (h r) -> p h r", h=H).unsqueeze(1).to_broadcast([P, m, H, P]),
                    in1=tables_t[:, rows, slot * P : (slot + 1) * P].unsqueeze(2).to_broadcast([P, m, H, P]),
                    op=MULT,
                )
            else:
                engine.tensor_tensor(
                    out=out,
                    in0=source.unsqueeze(1).to_broadcast([P, m, c1 - c0]),
                    in1=tables_t[:, rows, slot * P + c0 : slot * P + c1],
                    op=MULT,
                )

        def multiply_k_on_vector(unit):
            acc, end = unit["k_bank"], turned_tiles(unit) * P
            split = end - gpsimd_columns(unit)
            if split > 0:
                multiply_turned(unit, acc[:, 0:split], slice(0, 2), 0, split, nc.vector)
            if end < GROUP * P:
                turned = turned_tiles(unit)
                n = GROUP - turned
                slots = slice(unit["group"]["slot"] + turned, unit["group"]["slot"] + GROUP)
                halves = acc[:, end:].rearrange("p (i s d) -> p i s d", i=n, s=2)
                for s in range(2):
                    nc.vector.tensor_tensor(
                        out=products_of_half(unit["straight"], n, s),
                        in0=halves[:, :, s, :].unsqueeze(1).to_broadcast([P, 2, n, HALF]),
                        in1=tables[:, :, slots, s * HALF : (s + 1) * HALF],
                        op=MULT,
                    )

        def multiply_k_on_gpsimd(unit):
            end = turned_tiles(unit) * P
            split = end - gpsimd_columns(unit)
            if split < end:
                k_copy = stage.tile([P, GROUP * P], F32)
                nc.scalar.copy(out=k_copy[:, 0 : end - split], in_=unit["k_bank"][:, split:end])
                multiply_turned(unit, k_copy[:, 0 : end - split], slice(0, 2), split, end, nc.gpsimd)

        def add_turned(unit):
            group, turned = unit["group"], turned_tiles(unit)
            if unit["part"] == 0:
                group["k_sb"] = kresults.tile([P, GROUP, D], F32, name="k_sb")
            if turned == 0:
                return
            ko = psum.tile([P, turned, P], F32, name="ko")
            for i in range(turned):
                columns = slice(i * P, (i + 1) * P)
                for row, matrix in ((0, identity), (1, swap)):
                    nc.tensor.matmul(
                        ko[:, i, :],
                        lhsT=unit["k_parts"][:, row, columns],
                        rhs=matrix[:],
                        start=row == 0,
                        stop=row == 1,
                        is_transpose=True,
                    )
            if group["tiles"] == 1:
                nc.scalar.copy(out=group["k_sb"][:, 0, :].rearrange("p (h d) -> p h d", h=H), in_=ko[:])
            else:
                head = slice(unit["part"] * HD, (unit["part"] + 1) * HD)
                nc.scalar.copy(out=group["k_sb"][:, 0:turned, head], in_=ko[:])

        def add_straight(unit):
            turned, part = turned_tiles(unit), unit["part"]
            if turned < GROUP:
                n = GROUP - turned
                by_cos, by_sin = (
                    unit["straight"][:, w * ROW : w * ROW + n * HD].rearrange("p (i d) -> p i d", i=n) for w in range(2)
                )
                nc.gpsimd.tensor_tensor(
                    out=unit["group"]["k_sb"][:, turned:, part * HD : (part + 1) * HD], in0=by_cos, in1=by_sin, op=ADD
                )

        def products_of_half(parts, n, s):
            start = s * HALF
            step = ROW + HALF * (1 - 2 * s)
            both = parts[:, start : start + 2 * step].rearrange("p (w c) -> p w c", w=2)
            return both[:, :, 0 : n * HD].rearrange("p w (h d) -> p w h d", h=n)[:, :, :, 0:HALF]

        def start_q(unit):
            acc = psum.tile([P, D], F32, name="q_bank")
            project(unit, Q, acc)
            unit["q_bank"] = acc

        def multiply_q(unit):
            i = unit["part"] % PAIR
            if i == 0:
                unit["group"]["q_parts"] = results.tile([P, PAIR * 2 * ROW + HD], F32, name="q_parts")
            slot = unit["group"]["slot"] + unit["part"]
            halves = unit["q_bank"][:].rearrange("p (h s d) -> p h s d", h=H, s=2)
            for s in range(2):
                nc.vector.tensor_tensor(
                    out=products_of_half(unit["group"]["q_parts"][:, i * 2 * ROW :], H, s),
                    in0=halves[:, :, s, :].unsqueeze(1).to_broadcast([P, 2, H, HALF]),
                    in1=tables[:, :, slot, s * HALF : (s + 1) * HALF].unsqueeze(2).to_broadcast([P, 2, H, HALF]),
                    op=MULT,
                )

        def add_q(unit, engine, m):
            by_cos, by_sin = q_rows(unit, m)
            engine.tensor_tensor(out=by_cos, in0=by_cos, in1=by_sin, op=ADD)

        def q_rows(unit, m):
            i1 = unit["part"] % PAIR + 1
            rows = unit["group"]["q_parts"][:, 0 : PAIR * 2 * ROW].rearrange("p (i w c) -> p i w c", w=2, c=ROW)
            return [rows[:, i1 - m : i1, w, 0:D] for w in range(2)]

        def store_q(unit, m):
            store(unit, out_0, q_rows(unit, m)[0], m)

        def project_v(unit):
            i = unit["part"] % PAIR
            if i == 0:
                unit["group"]["v_sb"] = results.tile([P, PAIR, D], F32, name="v_sb")
            acc = psum.tile([P, D], F32, name="misc")
            project(unit, V, acc)
            nc.scalar.copy(out=unit["group"]["v_sb"][:, i, :], in_=acc[:])

        def store(unit, out, result, m):
            group, n = unit["group"], unit["group"]["tiles"]
            i1 = unit["part"] + 1
            for b, row in group["stores"]:
                nc.sync.dma_start(
                    out=out[b, row : row + n * P].rearrange("(p j) h d -> p j (h d)", j=n)[:, i1 - m : i1, :],
                    in_=result,
                )

        def store_heads(group, h0, h1):
            n = group["tiles"]
            for b, row in group["stores"]:
                nc.sync.dma_start(
                    out=out_1[b, row : row + n * P].rearrange("(p j) h d -> p j (h d)", j=n)[:, :, h0 * HD : h1 * HD],
                    in_=group["k_sb"][:, 0:n, h0 * HD : h1 * HD],
                )

        def keep_warm(count):
            for repeat in range(count):
                unused = psum.tile([P, D], F32, name="k_bank")
                nc.tensor.matmul(unused[:], lhsT=zeros[:, 0:P], rhs=zeros[:], start=True, stop=True)

        nc.vector.memset(zeros[:], 0.0)
        first, begin = groups[0], units[0]
        group_weight(Q, 0, D // 2, nc.vector.tensor_copy)
        keep_warm(4)
        transpose_tokens(first, 0)
        prepare_tables(first)
        group_weight(Q, 256, 384, nc.vector.tensor_copy)
        group_weight(Q, 384, D, nc.scalar.copy)
        quantise_tokens(first)
        quantise_weights(Q)
        group_weight(K, 0, 256, nc.vector.tensor_copy)
        group_weight(K, 256, D, nc.scalar.copy)
        keep_warm(2)
        transpose_tables(first)
        keep_warm(2)
        start_q(begin)
        multiply_q(begin)
        prepare_tables(groups[1])
        transpose_tokens(groups[1], 0, PAIR)
        transpose_tokens(groups[1], PAIR, PAIR, "ko")
        keep_warm(2)
        quantise_weights(K)
        start_k(begin)
        group_weight(V, 0, 320, nc.vector.tensor_copy)
        group_weight(V, 320, D, nc.scalar.copy)
        transpose_tables(groups[1])
        keep_warm(2)
        quantise_tokens(groups[1])
        start_k(units[1])
        start_q(units[1])
        multiply_k_on_gpsimd(units[1])
        multiply_k_on_vector(begin)
        multiply_k_on_vector(units[1])
        quantise_weights(V)

        for number in range(1, len(units)):
            unit, before = units[number], units[number - 1]
            following = units[number + 1] if number + 1 < len(units) else None
            group, part = unit["group"], unit["part"]
            next_group = groups[unit["index"] + 1] if unit["index"] + 1 < len(groups) else None
            second_group = groups[unit["index"] + 2] if unit["index"] + 2 < len(groups) else None
            last_group = next_group is None

            if number > 1:
                multiply_k_on_vector(unit)
            if following is not None:
                start_k(following)
                start_q(following)
                multiply_k_on_gpsimd(following)
            if number == 1:
                add_q(begin, nc.gpsimd, 1)
                store_q(begin, 1)
            if number == 1:
                transpose_tokens(groups[2], 0, PAIR)
                prepare_tables(groups[2])
                project_v(begin)
                store(begin, out_2, first["v_sb"][:, 0:1, :], 1)
            project_v(unit)
            if last_group:
                store(unit, out_2, group["v_sb"][:, part % PAIR : part % PAIR + 1, :], 1)
            elif part % PAIR == PAIR - 1:
                store(unit, out_2, group["v_sb"][:], PAIR)
            multiply_q(unit)
            if part == 2 and next_group is not None:
                quantise_tokens(next_group)
            add_turned(before)
            if number == 1:
                store_heads(first, 0, H)
            elif before["part"] == GROUP - 1:
                store_heads(before["group"], PAIR if before["group"] is groups[-2] else 0, H)
            if number == 1:
                transpose_tokens(groups[2], PAIR, PAIR)
            elif number > 2 and part < PAIR and next_group is not None:
                transpose_tokens(next_group, part + PAIR)
            if part >= PAIR and second_group is not None:
                transpose_tokens(second_group, part - PAIR)
            if part == 1 and next_group is not None and next_group["loads_tables"]:
                transpose_tables(next_group)
            if part == 2 and second_group is not None and second_group["loads_tables"]:
                prepare_tables(second_group)
            if part == PAIR and (last_group or group is groups[-2]):
                store_heads(group, 0, PAIR)
            if following is None:
                store_heads(group, 2, 3)
                add_turned(unit)
                store_heads(group, 3, H)
            add_straight(unit)
            add_q(unit, nc.vector if following is None else nc.gpsimd, 1)
            if last_group or part % PAIR == PAIR - 1:
                store_q(unit, 1 if last_group else PAIR)
